import numpy as np
import ml_dtypes


def mxq(x, axis, fmt="e4m3"):
    dtype, down = {"e4m3": (ml_dtypes.float8_e4m3fn, 7), "e5m2": (ml_dtypes.float8_e5m2, 14)}[fmt]
    v = np.moveaxis(np.asarray(x, np.float32).astype(ml_dtypes.bfloat16).astype(np.float64), axis, -1)
    blocks = v.reshape(v.shape[:-1] + (-1, 32))
    amax = np.abs(blocks).max(-1, keepdims=True)
    byte = np.maximum(np.where(amax > 0, np.frexp(amax)[1] - 1 + 127, 0) - down, 1)
    scale = np.exp2(byte - 127.0)
    codes = (blocks / scale).astype(np.float32).astype(dtype).astype(np.float64)
    return np.moveaxis((codes * scale).reshape(v.shape), -1, axis)


WIDE = False


def mx_kscale(k):
    if not WIDE:
        return np.ones(k)
    levels = np.array([10, -10, 5, -5, 0])
    if k % 512:
        return np.exp2(np.random.permutation(np.resize(levels, k // 32))).repeat(32)
    a = np.empty((k // 512, 16))
    for p in range(k // 512):
        a[p, :8] = np.random.permutation(np.resize(levels, 8))
        for g in range(8):
            far = levels[np.abs(levels - a[p, g]) >= 10]
            a[p, g + 8] = far[np.random.randint(len(far))]
    return np.exp2(a.ravel()).repeat(32)


BF16 = ml_dtypes.bfloat16


def bf(x):
    return np.asarray(x, np.float32).astype(BF16)


def f64(x):
    return np.asarray(x).astype(np.float64)


B, C, M, O, H, W = 4, 512, 512, 512, 32, 32
H2, W2 = H // 2, W // 2
KS = 3
PAD = KS // 2
BN_EPS = 1e-5


def haar_ll(x):
    a = x[:, :, 0::2, 0::2]
    b = x[:, :, 0::2, 1::2]
    c = x[:, :, 1::2, 0::2]
    d = x[:, :, 1::2, 1::2]
    return (a + b + c + d) * 0.5


def windows(u):
    up = np.pad(u, ((0, 0), (0, 0), (PAD, PAD), (PAD, PAD)))
    return np.stack([up[:, :, i:i + H2, j:j + W2] for i in range(KS) for j in range(KS)], axis=-1)


def draw0():
    s, t = mx_kscale(C), mx_kscale(M)
    return {
        "x": bf(np.random.standard_normal((B, C, H, W)) * s[None, :, None, None]),
        "w_c1": bf(np.random.standard_normal((M, C)) / np.sqrt(C) * t[:, None] / s[None, :]),
        "b_c1": bf(np.random.standard_normal(M) * 0.3 * t),
        "w_q": bf(np.random.standard_normal((O, M)) / np.sqrt(M) / t[None, :]),
        "w_k": bf(np.random.standard_normal((O, M)) / np.sqrt(M) / t[None, :]),
        "w_v": bf(np.random.standard_normal((O, M)) / np.sqrt(M) / t[None, :]),
        "bn_gamma": bf(1.0 + 0.1 * np.random.standard_normal(O)),
        "bn_beta": bf(0.3 * np.random.standard_normal(O)),
        "prelu_a": bf(np.random.uniform(0.15, 0.35, (1,))),
    }


def core(x, w_c1, b_c1, w_q, w_k, w_v, bn_gamma, bn_beta, prelu_a):
    ll = haar_ll(f64(x)).reshape(B, C, H2 * W2)
    y = (mxq(f64(w_c1), 1, "e4m3") @ mxq(ll, 1, "e4m3")) + f64(b_c1)[None, :, None]
    yq = mxq(y, 1, "e4m3")
    q = (mxq(f64(w_q), 1, "e4m3") @ yq).reshape(B, O, H2, W2)
    k = (mxq(f64(w_k), 1, "e4m3") @ yq).reshape(B, O, H2, W2)
    v = (mxq(f64(w_v), 1, "e4m3") @ yq).reshape(B, O, H2, W2)
    kw = windows(k)
    vw = windows(v)
    z = q[..., None] * kw
    e = np.exp(z - z.max(-1, keepdims=True))
    attn = e / e.sum(-1, keepdims=True)
    att = (attn * vw).sum(-1)
    m = att.mean(axis=(0, 2, 3), keepdims=True)
    var = att.var(axis=(0, 2, 3), keepdims=True)
    n = f64(bn_gamma)[None, :, None, None] * (att - m) / np.sqrt(var + BN_EPS) + f64(bn_beta)[None, :, None, None]
    return np.where(n >= 0, n, f64(prelu_a) * n)


def e4m3fn_bytes(y):
    return np.clip(np.asarray(y, np.float64), -448.0, 448.0).astype(np.float32).astype(ml_dtypes.float8_e4m3fn).view(np.uint8)


def e4m3fn_values(b):
    return np.asarray(b, np.uint8).view(ml_dtypes.float8_e4m3fn).astype(np.float64)


def setup_inputs():
    d = draw0()
    x0 = np.asarray(d['w_v']).astype(np.float64)
    s = (np.max(np.abs(x0), axis=(0,), keepdims=True) / 448.0).astype(np.float32)
    out = {}
    for k, v in d.items():
        if k == 'w_v':
            out['w_v_bytes'] = e4m3fn_bytes(x0 / s.astype(np.float64))
            out['w_v_scale'] = s
        else:
            out[k] = v
    return out


def reference(x, w_c1, b_c1, w_q, w_k, w_v_bytes, w_v_scale, bn_gamma, bn_beta, prelu_a):
    return core(x, w_c1, b_c1, w_q, w_k, e4m3fn_values(w_v_bytes) * w_v_scale.astype(np.float64), bn_gamma, bn_beta, prelu_a)

@@ -1,0 +1,525 @@
+from contextlib import ExitStack
+
+import concourse.mybir as mybir
+from concourse.masks import make_identity
+
+B, C, M, O = 4, 512, 512, 512
+NPX = 256
+P = 128
+T = 4
+FLOPS = 2 * B * NPX * C * M * 4 + B * O * NPX * 9 * 6
+
+F32 = mybir.dt.float32
+BF16 = mybir.dt.bfloat16
+U32 = mybir.dt.uint32
+I32 = mybir.dt.int32
+U8 = mybir.dt.uint8
+FP8 = mybir.dt.float8_e4m3fn
+FP8X4 = mybir.dt.float8_e4m3fn_x4
+ALU = mybir.AluOpType
+ACT = mybir.ActivationFunctionType
+
+OFFSETS = [(di, dj) for di in (-1, 0, 1) for dj in (-1, 0, 1)]
+NOFF = 9
+SB_ORDER = [(0, 0), (1, 0), (2, 0), (0, 1), (1, 1), (2, 1), (3, 0), (3, 1)]
+Z_ON_VECTOR = (4,)
+HW = 512
+
+
+def tile_merge_pa_kernel(tc, x, w_c1, b_c1, w_q, w_k, w_v_bytes, w_v_scale, bn_gamma, bn_beta, prelu_a, out):
+    nc = tc.nc
+    with ExitStack() as ctx:
+        keep = ctx.enter_context(tc.tile_pool(name="keep", bufs=1))
+        raws = ctx.enter_context(tc.tile_pool(name="raws", bufs=1))
+        work = ctx.enter_context(tc.tile_pool(name="work", bufs=2))
+        attn = ctx.enter_context(tc.tile_pool(name="attn", bufs=4))
+        pzk = ctx.enter_context(tc.psum_pool(name="pzk", bufs=3))
+        pv = ctx.enter_context(tc.psum_pool(name="pv", bufs=2))
+        psa = ctx.enter_context(tc.psum_pool(name="psa", bufs=3))
+        ctx.enter_context(tc.manual_schedule())
+
+        xs = []
+        for b in range(B):
+            xb = raws.tile([P, T, 1024], BF16, name="x%d" % b)
+            xs.append(xb)
+        xviews = [x[b].rearrange("(p t) h w -> p t (h w)", t=T) for b in range(B)]
+
+        def load_x(b):
+            for tt in range(2):
+                nc.sync.dma_start(out=xs[b][:, 2 * tt : 2 * tt + 2, :], in_=xviews[b][:, 2 * tt : 2 * tt + 2, :])
+
+        def load_w(ap, name):
+            raw = raws.tile([P, T, 512], BF16, name=name)
+            nc.sync.dma_start(out=raw[:], in_=ap.rearrange("(p t) k -> p t k", t=T))
+            return raw
+
+        load_x(0)
+        load_x(1)
+        raw_c1 = load_w(w_c1, "raw_c1")
+        b1 = keep.tile([P, T], BF16, name="b1")
+        nc.sync.dma_start(out=b1[:], in_=b_c1.rearrange("(p t) -> p t", t=T))
+        raw_k = load_w(w_k, "raw_k")
+        raw_q = load_w(w_q, "raw_q")
+        raw_vb = raws.tile([P, T, 512], U8, name="raw_vb")
+        nc.sync.dma_start(out=raw_vb[:], in_=w_v_bytes.rearrange("(p t) k -> p t k", t=T))
+        vscale = raws.tile([P, 512], F32, name="vscale")
+        nc.sync.dma_start(out=vscale[:], in_=w_v_scale.rearrange("o k -> (o k)").partition_broadcast(P))
+        load_x(2)
+        load_x(3)
+        gam_b = keep.tile([P, T], BF16, name="gam_b")
+        bet_b = keep.tile([P, T], BF16, name="bet_b")
+        a_b = keep.tile([P, 1], BF16, name="a_b")
+        nc.sync.dma_start(out=gam_b[:], in_=bn_gamma.rearrange("(p t) -> p t", t=T))
+        nc.sync.dma_start(out=bet_b[:], in_=bn_beta.rearrange("(p t) -> p t", t=T))
+        nc.sync.dma_start(out=a_b[:], in_=prelu_a.partition_broadcast(P))
+
+        ident_b = keep.tile([P, P], BF16, name="ident_b")
+        make_identity(nc, ident_b[:])
+        ident_f = keep.tile([P, P], F32, name="ident_f")
+        make_identity(nc, ident_f[:])
+
+        sp = keep.tile([P, NOFF, 1024], U8, name="sp", align_bytes=64)
+        nc.vector.memset(sp[:].rearrange("p o n -> p (o n)").bitcast(I32), 0)
+        ys = {}
+        for dj in (-1, 0, 1):
+            y_t = keep.tile([P, B, 288], U32, name="ys%d" % (dj + 1), align_bytes=64)
+            nc.vector.memset(y_t[:].rearrange("p b n -> p (b n)").bitcast(I32), 0)
+            ys[dj] = y_t
+        kpad, kb1, hmx, hmn = [], [], [], []
+        for par in range(2):
+            kp_t = keep.tile([P, 2, 18, 24], F32, name="kpad%d" % par)
+            nc.vector.memset(kp_t[:], 0.0)
+            kpad.append(kp_t)
+            kb_t = keep.tile([P, 2, 16, 20], BF16, name="kb1_%d" % par)
+            nc.vector.memset(kb_t[:], 0.0)
+            kb1.append(kb_t)
+            hx_t = keep.tile([P, 2, 18, 16], BF16, name="hmx%d" % par)
+            nc.vector.memset(hx_t[:], 0.0)
+            hmx.append(hx_t)
+            hn_t = keep.tile([P, 2, 18, 16], BF16, name="hmn%d" % par)
+            nc.vector.memset(hn_t[:], 0.0)
+            hmn.append(hn_t)
+        neghalf = keep.tile([P, 1], F32, name="neghalf")
+        nc.vector.memset(neghalf[:], -0.5)
+
+        def prep_weight(words, name, copy):
+            codes = keep.tile([P, 512], U32, name=name + "_codes", align_bytes=64)
+            scales = keep.tile([P, 512], U8, name=name + "_scales", align_bytes=64)
+            grouped = work.tile([P, 512, 4], BF16, name="grouped", align_bytes=64)
+            gw = grouped[:].rearrange("p n j -> p (n j)").bitcast(F32)
+            for half in range(2):
+                bank = psa.tile([P, 2, 2, P], F32, name="wbank", tag="sa")
+                for tt in range(2):
+                    t = 2 * half + tt
+                    for u in range(2):
+                        nc.tensor.transpose(bank[:, tt, u, :], words[:, 256 * t + u : 256 * (t + 1) : 2], ident_f[:])
+                copy(
+                    out=gw[:, 512 * half : 512 * (half + 1)].rearrange("p (t r u) -> p t r u", t=2, u=2),
+                    in_=bank[:].rearrange("p t u r -> p t r u"),
+                )
+            nc.vector.quantize_mx(out=codes[:].bitcast(FP8X4), scales=scales[:], in_=grouped[:].rearrange("p n j -> p (n j)"))
+            return codes, scales
+
+        def as_words(raw):
+            return raw[:].rearrange("p t k -> p (t k)").bitcast(F32)
+
+        llc = keep.tile([P, 1024], U32, name="llc", align_bytes=64)
+        lls = keep.tile([P, 1024], U8, name="lls", align_bytes=64)
+        ll_bf = [None] * B
+
+        def haar_pe(b):
+            lb = work.tile([P, NPX, 4], BF16, name="ll_bf", tag="ll_bf", align_bytes=64)
+            ll_bf[b] = lb
+            for h in range(2):
+                bank = pzk.tile([P, T, P], F32, name="hbank", tag="zk")
+                for t in range(T):
+                    view = xs[b][:, t, :].rearrange("p (i r w c) -> p i r w c", r=2, w=16, c=2)
+                    for n, (r, c) in enumerate(((0, 0), (0, 1), (1, 0), (1, 1))):
+                        nc.tensor.matmul(
+                            bank[:, t, :].rearrange("p (i w) -> p i w", w=16),
+                            lhsT=ident_b[:],
+                            rhs=view[:, 8 * h : 8 * h + 8, r, :, c],
+                            start=(n == 0),
+                            stop=(n == 3),
+                        )
+                nc.scalar.activation(
+                    out=lb[:, P * h : P * (h + 1), :], in_=bank[:].rearrange("p t n -> p n t"), func=ACT.Copy, scale=0.5
+                )
+
+        def haar_rows(b, eng, t0, t1, hr, lo):
+            xv = xs[b][:].rearrange("p t (i r w) -> p (t i) r w", r=2, w=32)
+            s = slice(16 * t0, 16 * t1)
+            eng.tensor_tensor(out=hr[:, s, :], in0=xv[:, s, 0, :], in1=xv[:, s, 1, :], op=ALU.add)
+            eng.tensor_tensor(out=lo[:, s, :], in0=hr[:, s, 0::2], in1=hr[:, s, 1::2], op=ALU.add)
+
+        haar_tiles = {}
+
+        def haar_alloc(b):
+            hr = work.tile([P, 64, 32], F32, name="hr", tag="hr", bufs=1)
+            lo = work.tile([P, 64, 16], F32, name="lo", tag="lo")
+            haar_tiles[b] = (hr, lo)
+
+        def haar_part(b, eng, t0, t1):
+            haar_rows(b, eng, t0, t1, *haar_tiles[b])
+
+        def haar_group(b):
+            lb = work.tile([P, NPX, 4], BF16, name="ll_bf", tag="ll_bf", align_bytes=64)
+            ll_bf[b] = lb
+            lo = haar_tiles[b][1]
+            nc.scalar.activation(
+                out=lb[:], in_=lo[:].rearrange("p (t i) w -> p (i w) t", t=T), func=ACT.Copy, scale=0.5
+            )
+
+        def quant_ll(b):
+            s = slice(NPX * b, NPX * (b + 1))
+            nc.vector.quantize_mx(
+                out=llc[:, s].bitcast(FP8X4), scales=lls[:, s], in_=ll_bf[b][:].rearrange("p n j -> p (n j)")
+            )
+
+        y_bf = [None] * B
+
+        def conv1(b):
+            yb = work.tile([P, NPX, 4], BF16, name="y_bf", tag="y_bf", align_bytes=64)
+            y_bf[b] = yb
+            for h in range(2):
+                bank = pzk.tile([P, T, P], F32, name="ybank", tag="zk")
+                px = slice(NPX * b + P * h, NPX * b + P * (h + 1))
+                for t in range(T):
+                    ch = slice(P * t, P * (t + 1))
+                    nc.tensor.matmul_mx(
+                        out=bank[:, t, :],
+                        lhsT=c1_codes[:, ch].bitcast(FP8X4),
+                        lhsT_scale=c1_scales[:, ch],
+                        rhs=llc[:, px].bitcast(FP8X4),
+                        rhs_scale=lls[:, px],
+                        start=True,
+                        stop=True,
+                    )
+                nc.vector.tensor_tensor(
+                    out=yb[:, P * h : P * (h + 1), :],
+                    in0=bank[:].rearrange("p t n -> p n t"),
+                    in1=b1[:].unsqueeze(1).to_broadcast([P, P, T]),
+                    op=ALU.add,
+                )
+
+        CENTER = 4
+
+        def quant_y(b):
+            nc.vector.quantize_mx(
+                out=ys[0][:, b, 16:272].bitcast(FP8X4),
+                scales=sp[:, CENTER, NPX * b : NPX * (b + 1)],
+                in_=y_bf[b][:].rearrange("p n j -> p (n j)"),
+            )
+
+        def shift_codes(half):
+            bs = slice(2 * half, 2 * half + 2)
+            src = ys[0][:, bs, 16:272].bitcast(I32).rearrange("p b (i w) -> p b i w", w=16)
+            for dj in (-1, 1):
+                dst = ys[dj][:, bs, 16:272].bitcast(I32).rearrange("p b (i w) -> p b i w", w=16)
+                lo, hi = max(0, -dj), min(16, 16 - dj)
+                nc.vector.tensor_copy(out=dst[:, :, :, lo:hi], in_=src[:, :, :, lo + dj : hi + dj])
+
+        def shift_scales(half):
+            px = slice(512 * half, 512 * (half + 1))
+            for dj in (-1, 1):
+                lo, hi = max(0, -dj), min(16, 16 - dj)
+                dst = sp[:, 4 + dj, px].rearrange("p (n w) -> p n w", w=16)
+                src = sp[:, CENTER, px].rearrange("p (n w) -> p n w", w=16)
+                nc.vector.tensor_copy(out=dst[:, :, lo:hi], in_=src[:, :, lo + dj : hi + dj])
+            for dj in (-1, 0, 1):
+                src = sp[:, 4 + dj, px].bitcast(I32).rearrange("p (b n) -> p b n", b=2)
+                for di in (-1, 1):
+                    dst = sp[:, 4 + 3 * di + dj, px].bitcast(I32).rearrange("p (b n) -> p b n", b=2)
+                    lo, hi = max(0, -4 * di), min(64, 64 - 4 * di)
+                    nc.vector.tensor_copy(out=dst[:, :, lo:hi], in_=src[:, :, lo + 4 * di : hi + 4 * di])
+
+        nq_t, qb_t, kb0_t, m_t, mparts = {}, {}, {}, {}, {}
+
+        def qk_matmul(bank, codes, scales, ct, half):
+            ch = slice(P * ct, P * (ct + 1))
+            for bb in range(2):
+                b = 2 * half + bb
+                nc.tensor.matmul_mx(
+                    out=bank[:, NPX * bb : NPX * (bb + 1)],
+                    lhsT=codes[:, ch].bitcast(FP8X4),
+                    lhsT_scale=scales[:, ch],
+                    rhs=ys[0][:, b, 16:272].bitcast(FP8X4),
+                    rhs_scale=sp[:, CENTER, NPX * b : NPX * (b + 1)],
+                    start=True,
+                    stop=True,
+                )
+
+        def make_k(g):
+            ct, half = SB_ORDER[g]
+            bank = pzk.tile([P, HW], F32, name="kbank", tag="zk")
+            qk_matmul(bank, k_codes, k_scales, ct, half)
+            bv = bank[:].rearrange("p (b i w) -> p b i w", b=2, w=16)
+            nc.scalar.copy(out=kpad[g % 2][:, :, 1:17, 4:20], in_=bv)
+            kb0 = attn.tile([P, 2, 16, 16], BF16, name="kb0", tag="kb0", bufs=2)
+            kb0_t[g] = kb0
+            nc.scalar.copy(out=kb0[:].rearrange("p b i w -> p (b i w)"), in_=bank[:])
+            nc.scalar.copy(out=kb1[g % 2][:, :, :, 3:19], in_=kb0[:])
+
+        def make_q(g):
+            ct, half = SB_ORDER[g]
+            bank = pzk.tile([P, HW], F32, name="qbank", tag="zk")
+            qk_matmul(bank, q_codes, q_scales, ct, half)
+            nq = attn.tile([P, HW], F32, name="nq", tag="nq", bufs=2)
+            qb = attn.tile([P, HW], BF16, name="qb", tag="qb", bufs=2)
+            nq_t[g], qb_t[g] = nq, qb
+            nc.scalar.activation(out=nq[:], in_=bank[:], func=ACT.Copy, scale=-1.0)
+            nc.scalar.copy(out=qb[:], in_=bank[:])
+
+        def make_ext(g, which):
+            op = ALU.max if which == 0 else ALU.min
+            hx = (hmx if which == 0 else hmn)[g % 2]
+            k1 = kb1[g % 2]
+            tmp = attn.tile([P, 2, 16, 16], BF16, name="tmp", tag="tmp", bufs=2)
+            nc.vector.tensor_tensor(out=tmp[:], in0=k1[:, :, :, 2:18], in1=k1[:, :, :, 4:20], op=op)
+            nc.vector.tensor_tensor(out=hx[:, :, 1:17, :], in0=tmp[:], in1=kb0_t[g][:], op=op)
+            tmp2 = attn.tile([P, 2, 16, 16], BF16, name="tmp2", tag="tmp2", bufs=2)
+            nc.vector.tensor_tensor(out=tmp2[:], in0=hx[:, :, 0:16, :], in1=hx[:, :, 1:17, :], op=op)
+            ext = attn.tile([P, 2, 16, 16], BF16, name="ext", tag="ext%d" % which, bufs=2)
+            nc.vector.tensor_tensor(out=ext[:], in0=tmp2[:], in1=hx[:, :, 2:18, :], op=op)
+            mparts[(g, which)] = ext
+
+        def make_m(g):
+            prods = []
+            for which in range(2):
+                pr = attn.tile([P, HW], BF16, name="pr", tag="pr%d" % which, bufs=2)
+                nc.vector.tensor_tensor(
+                    out=pr[:], in0=qb_t[g][:], in1=mparts[(g, which)][:].rearrange("p b i w -> p (b i w)"), op=ALU.mult
+                )
+                prods.append(pr)
+            mt = attn.tile([P, HW], F32, name="mt", tag="mt", bufs=2)
+            nc.vector.tensor_tensor(out=mt[:], in0=prods[0][:], in1=prods[1][:], op=ALU.max)
+            m_t[g] = mt
+
+        NS = NOFF * len(SB_ORDER)
+        z_t, zm_t, e_t, v_t, ev_t, sa_t = {}, {}, {}, {}, {}, {}
+
+        def step_z(s):
+            g, j = divmod(s, NOFF)
+            di, dj = OFFSETS[j]
+            zt = attn.tile([P, HW], F32, name="zt", tag="zt")
+            z_t[s] = zt
+            eng = nc.vector if j in Z_ON_VECTOR else nc.gpsimd
+            eng.tensor_tensor(
+                out=zt[:].rearrange("p (b i w) -> p b i w", b=2, w=16),
+                in0=nq_t[g][:].rearrange("p (b i w) -> p b i w", b=2, w=16),
+                in1=kpad[g % 2][:, :, 1 + di : 17 + di, 4 + dj : 20 + dj],
+                op=ALU.mult,
+            )
+
+        def add_transposed(dst, src, start, stop):
+            nc.tensor.matmul(dst, lhsT=src, rhs=ident_f[:], start=start, stop=stop, is_transpose=True)
+
+        def step_zm(s):
+            g = s // NOFF
+            bank = pzk.tile([P, HW], F32, name="zmbank", tag="zk")
+            zm_t[s] = bank
+            for n in range(4):
+                blk = slice(P * n, P * (n + 1))
+                add_transposed(bank[:, blk], z_t[s][:, blk], True, False)
+                add_transposed(bank[:, blk], m_t[g][:, blk], False, True)
+
+        def step_exp(s):
+            et = attn.tile([P, HW], F32, name="et", tag="et")
+            e_t[s] = et
+            nc.scalar.activation(out=et[:], in_=zm_t[s][:], func=ACT.Exp, scale=-1.0)
+
+        def step_v(s):
+            g, j = divmod(s, NOFF)
+            ct, half = SB_ORDER[g]
+            di, dj = OFFSETS[j]
+            bank = pv.tile([P, HW], F32, name="vbank", tag="v")
+            v_t[s] = bank
+            ch = slice(P * ct, P * (ct + 1))
+            for n in range(4):
+                b, r0 = 2 * half + n // 2, 8 * (n % 2)
+                w0 = 16 * (r0 + 1 + di)
+                px = NPX * b + 16 * r0
+                nc.tensor.matmul_mx(
+                    out=bank[:, P * n : P * (n + 1)],
+                    lhsT=ys[dj][:, b, w0 : w0 + P].bitcast(FP8X4),
+                    lhsT_scale=sp[:, 4 + 3 * di + dj, px : px + P],
+                    rhs=v_codes[:, ch].bitcast(FP8X4),
+                    rhs_scale=v_scales[:, ch],
+                    start=True,
+                    stop=True,
+                )
+
+        def step_ev(s):
+            evt = attn.tile([P, HW], F32, name="evt", tag="evt")
+            ev_t[s] = evt
+            nc.vector.tensor_tensor(out=evt[:], in0=v_t[s][:], in1=e_t[s][:], op=ALU.mult)
+
+        def step_sa(s):
+            g, j = divmod(s, NOFF)
+            if j == 0:
+                sbank = psa.tile([P, HW], F32, name="sbank", tag="sa")
+                abank = psa.tile([P, HW], F32, name="abank", tag="sa")
+                sa_t[g] = (sbank, abank)
+            for bank, src in zip(sa_t[g], (e_t[s], ev_t[s])):
+                for n in range(4):
+                    blk = slice(P * n, P * (n + 1))
+                    add_transposed(bank[:, blk], src[:, blk], j == 0 and n == 0, j == NOFF - 1 and n == 3)
+
+        ss_t, as_t, r_t, att_t, aff_t = {}, {}, {}, {}, {}
+        small = {}
+
+        def sums_out(g):
+            ct, half = SB_ORDER[g]
+            if ct not in ss_t:
+                ss = attn.tile([P, 1024], F32, name="ss", tag="ss", bufs=3)
+                as_ = attn.tile([P, 1024], F32, name="as_", tag="as", bufs=3)
+                ss_t[ct], as_t[ct] = ss, as_
+            sl = slice(HW * half, HW * (half + 1))
+            nc.scalar.copy(out=ss_t[ct][:, sl], in_=sa_t[g][0][:])
+            nc.scalar.copy(out=as_t[ct][:, sl], in_=sa_t[g][1][:])
+
+        def recip(ct):
+            ln = attn.tile([P, 1024], F32, name="ln", tag="ln", bufs=1)
+            nc.scalar.activation(out=ln[:], in_=ss_t[ct][:], func=ACT.Ln)
+            r = attn.tile([P, 1024], F32, name="r", tag="r", bufs=1)
+            nc.scalar.activation(out=r[:], in_=ln[:], func=ACT.Exp, scale=-1.0)
+            r_t[ct] = r
+
+        def normalise(ct):
+            at = attn.tile([P, 1024], F32, name="at", tag="at", bufs=2)
+            att_t[ct] = at
+            stats = attn.tile([P, 2, 6], F32, name="stats", tag="stats", bufs=2)
+            for h in range(2):
+                sl = slice(HW * h, HW * (h + 1))
+                nc.vector.tensor_tensor(out=at[:, sl], in0=as_t[ct][:, sl], in1=r_t[ct][:, sl], op=ALU.mult)
+            for h in range(2):
+                nc.vector.bn_stats(out=stats[:, h, :], in_=at[:, HW * h : HW * (h + 1)])
+            mv = attn.tile([P, 2], F32, name="mv", tag="mv", bufs=2)
+            nc.vector.bn_aggr(out=mv[:], in_=stats[:].rearrange("p h s -> p (h s)"))
+            small[ct] = mv
+
+        gam = keep.tile([P, T], F32, name="gam")
+        bet = keep.tile([P, T], F32, name="bet")
+        aa = keep.tile([P, 1], F32, name="aa")
+        oma = keep.tile([P, 1], F32, name="oma")
+
+        def affine(ct):
+            mv = small[ct]
+            cs = attn.tile([P, 8], F32, name="cs", tag="cs", bufs=2)
+            aff_t[ct] = cs
+            g_ = nc.gpsimd
+            g_.tensor_scalar(out=cs[:, 0:1], in0=mv[:, 1:2], scalar1=1.0, scalar2=1e-5, op0=ALU.mult, op1=ALU.add)
+            g_.tensor_tensor(out=cs[:, 1:2], in0=cs[:, 0:1], in1=neghalf[:], op=ALU.pow)
+            g_.tensor_tensor(out=cs[:, 2:3], in0=cs[:, 1:2], in1=gam[:, ct : ct + 1], op=ALU.mult)
+            g_.tensor_tensor(out=cs[:, 3:4], in0=cs[:, 2:3], in1=mv[:, 0:1], op=ALU.mult)
+            g_.tensor_tensor(out=cs[:, 4:5], in0=bet[:, ct : ct + 1], in1=cs[:, 3:4], op=ALU.subtract)
+            g_.tensor_tensor(out=cs[:, 5:6], in0=cs[:, 2:3], in1=aa[:], op=ALU.mult)
+            g_.tensor_tensor(out=cs[:, 6:7], in0=cs[:, 4:5], in1=aa[:], op=ALU.mult)
+
+        out_v = out.rearrange("b (p t) h w -> t p b (h w)", t=T)
+
+        def finish(ct):
+            cs, at = aff_t[ct], att_t[ct]
+            for h in range(2):
+                sl = slice(HW * h, HW * (h + 1))
+                re = attn.tile([P, HW], F32, name="re", tag="re", bufs=2)
+                li = attn.tile([P, HW], F32, name="li", tag="li", bufs=2)
+                res = attn.tile([P, HW], F32, name="res", tag="res", bufs=2)
+                nc.scalar.activation(out=re[:], in_=at[:, sl], func=ACT.Relu, scale=cs[:, 2:3], bias=cs[:, 4:5])
+                nc.scalar.activation(out=li[:], in_=at[:, sl], func=ACT.Identity, scale=cs[:, 5:6], bias=cs[:, 6:7])
+                nc.vector.scalar_tensor_tensor(
+                    out=res[:], in0=re[:], scalar=oma[:], in1=li[:], op0=ALU.mult, op1=ALU.add
+                )
+                nc.sync.dma_start(
+                    out=out_v[ct][:, 2 * h : 2 * h + 2, :], in_=res[:].rearrange("p (b n) -> p b n", b=2)
+                )
+
+        haar_pe(0)
+        haar_alloc(1)
+        haar_part(1, nc.gpsimd, 2, 4)
+        haar_part(1, nc.vector, 0, 2)
+        c1_codes, c1_scales = prep_weight(as_words(raw_c1), "c1", nc.scalar.copy)
+        quant_ll(0)
+        haar_group(1)
+        conv1(0)
+        k_codes, k_scales = prep_weight(as_words(raw_k), "wk", nc.scalar.copy)
+        quant_y(0)
+        quant_ll(1)
+        conv1(1)
+        q_codes, q_scales = prep_weight(as_words(raw_q), "wq", nc.scalar.copy)
+        quant_y(1)
+        make_k(0)
+        make_q(0)
+        make_ext(0, 0)
+        make_ext(0, 1)
+        make_m(0)
+        step_z(0)
+        step_z(1)
+        step_z(2)
+        wv_bf = raws.tile([P, T, 512], BF16, name="wv_bf")
+        for t in range(T):
+            nc.vector.tensor_tensor(out=wv_bf[:, t, :], in0=raw_vb[:, t, :].bitcast(FP8), in1=vscale[:], op=ALU.mult)
+        v_codes, v_scales = prep_weight(as_words(wv_bf), "wv", nc.scalar.copy)
+        shift_codes(0)
+        shift_scales(0)
+        nc.vector.tensor_copy(out=gam[:], in_=gam_b[:])
+        nc.vector.tensor_copy(out=bet[:], in_=bet_b[:])
+        nc.vector.tensor_copy(out=aa[:], in_=a_b[:])
+        nc.vector.tensor_scalar(out=oma[:], in0=aa[:], scalar1=-1.0, scalar2=1.0, op0=ALU.mult, op1=ALU.add)
+        step_zm(0)
+        step_exp(0)
+        step_v(0)
+        step_zm(1)
+        step_exp(1)
+        step_v(1)
+        step_ev(0)
+
+        extras = {}
+
+        def at_slot(i, fn, *args):
+            extras.setdefault(i, []).append((fn, args))
+
+        for n, b in enumerate((2, 3)):
+            base = 7 * n
+            at_slot(base, haar_alloc, b)
+            for t in range(T):
+                at_slot(base + t, haar_part, b, nc.vector, t, t + 1)
+            at_slot(base + 4, haar_group, b)
+            at_slot(base + 5, quant_ll, b)
+            at_slot(base + 5, conv1, b)
+            at_slot(base + 6, quant_y, b)
+        at_slot(15, shift_codes, 1)
+        at_slot(15, shift_scales, 1)
+
+        done = set()
+        for g, (ct, half) in enumerate(SB_ORDER):
+            s0 = NOFF * g
+            if g + 1 < len(SB_ORDER):
+                at_slot(s0 + 0, make_k, g + 1)
+                at_slot(s0 + 1, make_q, g + 1)
+                at_slot(s0 + 3, make_ext, g + 1, 0)
+                at_slot(s0 + 4, make_ext, g + 1, 1)
+                at_slot(s0 + 5, make_m, g + 1)
+            e0 = s0 + NOFF
+            at_slot(e0, sums_out, g)
+            if ct in done:
+                at_slot(e0 + 1, recip, ct)
+                at_slot(e0 + 2, normalise, ct)
+                at_slot(e0 + 3, affine, ct)
+                at_slot(e0 + 4, finish, ct)
+            done.add(ct)
+
+        for i in range(NS + NOFF):
+            if i + 2 < NS:
+                step_zm(i + 2)
+                step_exp(i + 2)
+            if i + 3 < NS:
+                step_z(i + 3)
+            if i + 1 < NS:
+                step_ev(i + 1)
+            if i < NS:
+                step_sa(i)
+            if i + 2 < NS:
+                step_v(i + 2)
+            for fn, args in extras.get(i, []):
+                fn(*args)

@@ -7,6 +7,7 @@ B, C, M, O = 4, 512, 512, 512
 NPX = 256
 P = 128
 T = 4
+HW = 512
 FLOPS = 2 * B * NPX * C * M * 4 + B * O * NPX * 9 * 6
 
 F32 = mybir.dt.float32
@@ -19,11 +20,34 @@ FP8X4 = mybir.dt.float8_e4m3fn_x4
 ALU = mybir.AluOpType
 ACT = mybir.ActivationFunctionType
 
-OFFSETS = [(di, dj) for di in (-1, 0, 1) for dj in (-1, 0, 1)]
+OFFSETS = [(di, dj) for dj in (0, 1, -1) for di in (0, 1, -1)]
 NOFF = 9
+CENTER = 4
 SB_ORDER = [(0, 0), (1, 0), (2, 0), (0, 1), (1, 1), (2, 1), (3, 0), (3, 1)]
-Z_ON_VECTOR = (4,)
-HW = 512
+L_X = 3
+L_Z = 5
+L_K = 6
+L_EV = 1
+L_V = 2
+E_K = -13
+E_QT = -12
+E_Q = -10
+E_CH = -10
+E_MT = -6
+F_LN = 2
+F_A = 3
+F_SQ = 7
+F_RS = 7
+F_CS = 9
+F_R = 12
+F_O = 14
+V_SUB = (5,)
+KEEP = 0
+LI_V = 0
+B_ZK = 3
+B_V = 3
+B_SA = 2
+N_PE_HAAR = 3
 
 
 def tile_merge_pa_kernel(tc, x, w_c1, b_c1, w_q, w_k, w_v_bytes, w_v_scale, bn_gamma, bn_beta, prelu_a, out):
@@ -32,30 +56,30 @@ def tile_merge_pa_kernel(tc, x, w_c1, b_c1, w_q, w_k, w_v_bytes, w_v_scale, bn_g
         keep = ctx.enter_context(tc.tile_pool(name="keep", bufs=1))
         raws = ctx.enter_context(tc.tile_pool(name="raws", bufs=1))
         work = ctx.enter_context(tc.tile_pool(name="work", bufs=2))
-        attn = ctx.enter_context(tc.tile_pool(name="attn", bufs=4))
-        pzk = ctx.enter_context(tc.psum_pool(name="pzk", bufs=3))
-        pv = ctx.enter_context(tc.psum_pool(name="pv", bufs=2))
-        psa = ctx.enter_context(tc.psum_pool(name="psa", bufs=3))
+        attn = ctx.enter_context(tc.tile_pool(name="attn", bufs=2))
+        pzk = ctx.enter_context(tc.psum_pool(name="pzk", bufs=B_ZK))
+        pv = ctx.enter_context(tc.psum_pool(name="pv", bufs=B_V))
+        psa = ctx.enter_context(tc.psum_pool(name="psa", bufs=B_SA))
         ctx.enter_context(tc.manual_schedule())
 
         xs = []
         for b in range(B):
             xb = raws.tile([P, T, 1024], BF16, name="x%d" % b)
             xs.append(xb)
-        xviews = [x[b].rearrange("(p t) h w -> p t (h w)", t=T) for b in range(B)]
 
         def load_x(b):
+            view = x[b].rearrange("(p t) h w -> p t (h w)", t=T)
             for tt in range(2):
-                nc.sync.dma_start(out=xs[b][:, 2 * tt : 2 * tt + 2, :], in_=xviews[b][:, 2 * tt : 2 * tt + 2, :])
+                nc.sync.dma_start(out=xs[b][:, 2 * tt : 2 * tt + 2, :], in_=view[:, 2 * tt : 2 * tt + 2, :])
 
         def load_w(ap, name):
             raw = raws.tile([P, T, 512], BF16, name=name)
             nc.sync.dma_start(out=raw[:], in_=ap.rearrange("(p t) k -> p t k", t=T))
             return raw
 
+        raw_c1 = load_w(w_c1, "raw_c1")
         load_x(0)
         load_x(1)
-        raw_c1 = load_w(w_c1, "raw_c1")
         b1 = keep.tile([P, T], BF16, name="b1")
         nc.sync.dma_start(out=b1[:], in_=b_c1.rearrange("(p t) -> p t", t=T))
         raw_k = load_w(w_k, "raw_k")
@@ -73,51 +97,53 @@ def tile_merge_pa_kernel(tc, x, w_c1, b_c1, w_q, w_k, w_v_bytes, w_v_scale, bn_g
         nc.sync.dma_start(out=bet_b[:], in_=bn_beta.rearrange("(p t) -> p t", t=T))
         nc.sync.dma_start(out=a_b[:], in_=prelu_a.partition_broadcast(P))
 
-        ident_b = keep.tile([P, P], BF16, name="ident_b")
-        make_identity(nc, ident_b[:])
         ident_f = keep.tile([P, P], F32, name="ident_f")
         make_identity(nc, ident_f[:])
-
-        sp = keep.tile([P, NOFF, 1024], U8, name="sp", align_bytes=64)
-        nc.vector.memset(sp[:].rearrange("p o n -> p (o n)").bitcast(I32), 0)
-        ys = {}
-        for dj in (-1, 0, 1):
-            y_t = keep.tile([P, B, 288], U32, name="ys%d" % (dj + 1), align_bytes=64)
-            nc.vector.memset(y_t[:].rearrange("p b n -> p (b n)").bitcast(I32), 0)
-            ys[dj] = y_t
-        kpad, kb1, hmx, hmn = [], [], [], []
+        ident_b = keep.tile([P, P], BF16, name="ident_b")
+        make_identity(nc, ident_b[:])
+        kb1, hmx, hmn = [], [], []
         for par in range(2):
-            kp_t = keep.tile([P, 2, 18, 24], F32, name="kpad%d" % par)
-            nc.vector.memset(kp_t[:], 0.0)
-            kpad.append(kp_t)
             kb_t = keep.tile([P, 2, 16, 20], BF16, name="kb1_%d" % par)
-            nc.vector.memset(kb_t[:], 0.0)
+            nc.gpsimd.memset(kb_t[:].rearrange("p b i w -> p (b i w)").bitcast(I32), 0)
             kb1.append(kb_t)
-            hx_t = keep.tile([P, 2, 18, 16], BF16, name="hmx%d" % par)
-            nc.vector.memset(hx_t[:], 0.0)
-            hmx.append(hx_t)
-            hn_t = keep.tile([P, 2, 18, 16], BF16, name="hmn%d" % par)
-            nc.vector.memset(hn_t[:], 0.0)
-            hmn.append(hn_t)
+            for lst, nm in ((hmx, "hmx"), (hmn, "hmn")):
+                h_t = keep.tile([P, 2, 18, 16], BF16, name="%s%d" % (nm, par))
+                nc.gpsimd.memset(h_t[:].rearrange("p b i w -> p (b i w)").bitcast(I32), 0)
+                lst.append(h_t)
+        sp = keep.tile([P, NOFF, 1024], U8, name="sp", align_bytes=64)
+        nc.gpsimd.memset(sp[:].rearrange("p o n -> p (o n)").bitcast(I32), 0)
+        ys = {}
+        for dj in (0, -1, 1):
+            y_t = keep.tile([P, B, 288], U32, name="ys%d" % (dj + 1), align_bytes=64)
+            nc.gpsimd.memset(y_t[:].rearrange("p b n -> p (b n)").bitcast(I32), 0)
+            ys[dj] = y_t
         neghalf = keep.tile([P, 1], F32, name="neghalf")
-        nc.vector.memset(neghalf[:], -0.5)
+        nc.gpsimd.memset(neghalf[:], -0.5)
 
-        def prep_weight(words, name, copy):
-            codes = keep.tile([P, 512], U32, name=name + "_codes", align_bytes=64)
-            scales = keep.tile([P, 512], U8, name=name + "_scales", align_bytes=64)
-            grouped = work.tile([P, 512, 4], BF16, name="grouped", align_bytes=64)
-            gw = grouped[:].rearrange("p n j -> p (n j)").bitcast(F32)
+        def tr_weight(words, name, pool, tag):
+            banks = []
             for half in range(2):
-                bank = psa.tile([P, 2, 2, P], F32, name="wbank", tag="sa")
+                bank = pool.tile([P, 2, 2, P], F32, name="wbank", tag=tag)
                 for tt in range(2):
                     t = 2 * half + tt
                     for u in range(2):
                         nc.tensor.transpose(bank[:, tt, u, :], words[:, 256 * t + u : 256 * (t + 1) : 2], ident_f[:])
-                copy(
+                banks.append(bank)
+            grouped = work.tile([P, 512, 4], BF16, name="grouped", align_bytes=64)
+            return name, banks, grouped
+
+        def copy_weight(w, copies):
+            gw = w[2][:].rearrange("p n j -> p (n j)").bitcast(F32)
+            for half in range(2):
+                copies[half](
                     out=gw[:, 512 * half : 512 * (half + 1)].rearrange("p (t r u) -> p t r u", t=2, u=2),
-                    in_=bank[:].rearrange("p t u r -> p t r u"),
+                    in_=w[1][half][:].rearrange("p t u r -> p t r u"),
                 )
-            nc.vector.quantize_mx(out=codes[:].bitcast(FP8X4), scales=scales[:], in_=grouped[:].rearrange("p n j -> p (n j)"))
+
+        def quant_weight(w):
+            codes = keep.tile([P, 512], U32, name=w[0] + "_codes", align_bytes=64)
+            scales = keep.tile([P, 512], U8, name=w[0] + "_scales", align_bytes=64)
+            nc.vector.quantize_mx(out=codes[:].bitcast(FP8X4), scales=scales[:], in_=w[2][:].rearrange("p n j -> p (n j)"))
             return codes, scales
 
         def as_words(raw):
@@ -125,49 +151,57 @@ def tile_merge_pa_kernel(tc, x, w_c1, b_c1, w_q, w_k, w_v_bytes, w_v_scale, bn_g
 
         llc = keep.tile([P, 1024], U32, name="llc", align_bytes=64)
         lls = keep.tile([P, 1024], U8, name="lls", align_bytes=64)
-        ll_bf = [None] * B
-
-        def haar_pe(b):
-            lb = work.tile([P, NPX, 4], BF16, name="ll_bf", tag="ll_bf", align_bytes=64)
-            ll_bf[b] = lb
-            for h in range(2):
-                bank = pzk.tile([P, T, P], F32, name="hbank", tag="zk")
-                for t in range(T):
-                    view = xs[b][:, t, :].rearrange("p (i r w c) -> p i r w c", r=2, w=16, c=2)
-                    for n, (r, c) in enumerate(((0, 0), (0, 1), (1, 0), (1, 1))):
-                        nc.tensor.matmul(
-                            bank[:, t, :].rearrange("p (i w) -> p i w", w=16),
-                            lhsT=ident_b[:],
-                            rhs=view[:, 8 * h : 8 * h + 8, r, :, c],
-                            start=(n == 0),
-                            stop=(n == 3),
-                        )
-                nc.scalar.activation(
-                    out=lb[:, P * h : P * (h + 1), :], in_=bank[:].rearrange("p t n -> p n t"), func=ACT.Copy, scale=0.5
-                )
-
-        def haar_rows(b, eng, t0, t1, hr, lo):
-            xv = xs[b][:].rearrange("p t (i r w) -> p (t i) r w", r=2, w=32)
-            s = slice(16 * t0, 16 * t1)
-            eng.tensor_tensor(out=hr[:, s, :], in0=xv[:, s, 0, :], in1=xv[:, s, 1, :], op=ALU.add)
-            eng.tensor_tensor(out=lo[:, s, :], in0=hr[:, s, 0::2], in1=hr[:, s, 1::2], op=ALU.add)
-
-        haar_tiles = {}
+        ll_bf, haar_tiles, hbank_t = {}, {}, {}
 
         def haar_alloc(b):
-            hr = work.tile([P, 64, 32], F32, name="hr", tag="hr", bufs=1)
-            lo = work.tile([P, 64, 16], F32, name="lo", tag="lo")
-            haar_tiles[b] = (hr, lo)
-
-        def haar_part(b, eng, t0, t1):
-            haar_rows(b, eng, t0, t1, *haar_tiles[b])
-
-        def haar_group(b):
             lb = work.tile([P, NPX, 4], BF16, name="ll_bf", tag="ll_bf", align_bytes=64)
             ll_bf[b] = lb
-            lo = haar_tiles[b][1]
+            hr = work.tile([P, 64, 32], F32, name="hr", tag="hr", bufs=1)
+            lo = work.tile([P, 64, 16], F32, name="lo", tag="lo", bufs=2)
+            haar_tiles[b] = (hr, lo)
+
+        def haar_pe(b, h):
+            bank = pzk.tile([P, T, P], F32, name="hbank", tag="zk")
+            for t in range(T):
+                view = xs[b][:, t, :].rearrange("p (i r w c) -> p i r w c", r=2, w=16, c=2)
+                for n, (r, c) in enumerate(((0, 0), (0, 1), (1, 0), (1, 1))):
+                    nc.tensor.matmul(
+                        bank[:, t, :].rearrange("p (i w) -> p i w", w=16),
+                        lhsT=ident_b[:],
+                        rhs=view[:, 8 * h : 8 * h + 8, r, :, c],
+                        start=(n == 0),
+                        stop=(n == 3),
+                    )
+            hbank_t[(b, h)] = bank
+
+        def haar_pe_out(b, h):
             nc.scalar.activation(
-                out=lb[:], in_=lo[:].rearrange("p (t i) w -> p (i w) t", t=T), func=ACT.Copy, scale=0.5
+                out=ll_bf[b][:, P * h : P * (h + 1), :],
+                in_=hbank_t[(b, h)][:].rearrange("p t n -> p n t"),
+                func=ACT.Copy,
+                scale=0.5,
+            )
+
+        def haar_v(b, h, t0=0, t1=T):
+            hr, lo = haar_tiles[b]
+            xv = xs[b][:].rearrange("p t (i r w) -> p t i r w", r=2, w=32)
+            hv = hr[:].rearrange("p (t i) w -> p t i w", t=T)
+            lv = lo[:].rearrange("p (t i) w -> p t i w", t=T)
+            s = slice(8 * h, 8 * h + 8)
+            nc.vector.tensor_tensor(
+                out=hv[:, t0:t1, s, :], in0=xv[:, t0:t1, s, 0, :], in1=xv[:, t0:t1, s, 1, :], op=ALU.add
+            )
+            nc.vector.tensor_tensor(
+                out=lv[:, t0:t1, s, :], in0=hv[:, t0:t1, s, 0::2], in1=hv[:, t0:t1, s, 1::2], op=ALU.add
+            )
+
+        def haar_group(b, h):
+            s = slice(8 * h, 8 * h + 8)
+            nc.scalar.activation(
+                out=ll_bf[b][:, P * h : P * (h + 1), :],
+                in_=haar_tiles[b][1][:].rearrange("p (t i) w -> p i w t", t=T)[:, s],
+                func=ACT.Copy,
+                scale=0.5,
             )
 
         def quant_ll(b):
@@ -176,33 +210,41 @@ def tile_merge_pa_kernel(tc, x, w_c1, b_c1, w_q, w_k, w_v_bytes, w_v_scale, bn_g
                 out=llc[:, s].bitcast(FP8X4), scales=lls[:, s], in_=ll_bf[b][:].rearrange("p n j -> p (n j)")
             )
 
-        y_bf = [None] * B
+        y_bf, ybank_t = {}, {}
 
-        def conv1(b):
-            yb = work.tile([P, NPX, 4], BF16, name="y_bf", tag="y_bf", align_bytes=64)
-            y_bf[b] = yb
-            for h in range(2):
-                bank = pzk.tile([P, T, P], F32, name="ybank", tag="zk")
-                px = slice(NPX * b + P * h, NPX * b + P * (h + 1))
-                for t in range(T):
-                    ch = slice(P * t, P * (t + 1))
-                    nc.tensor.matmul_mx(
-                        out=bank[:, t, :],
-                        lhsT=c1_codes[:, ch].bitcast(FP8X4),
-                        lhsT_scale=c1_scales[:, ch],
-                        rhs=llc[:, px].bitcast(FP8X4),
-                        rhs_scale=lls[:, px],
-                        start=True,
-                        stop=True,
-                    )
-                nc.vector.tensor_tensor(
-                    out=yb[:, P * h : P * (h + 1), :],
-                    in0=bank[:].rearrange("p t n -> p n t"),
-                    in1=b1[:].unsqueeze(1).to_broadcast([P, P, T]),
-                    op=ALU.add,
+        def conv1(b, h, bank):
+            if h == 0:
+                yb = work.tile([P, NPX, 4], BF16, name="y_bf", tag="y_bf", align_bytes=64)
+                y_bf[b] = yb
+            px = slice(NPX * b + P * h, NPX * b + P * (h + 1))
+            for t in range(T):
+                ch = slice(P * t, P * (t + 1))
+                nc.tensor.matmul_mx(
+                    out=bank[:, t, :],
+                    lhsT=c1_codes[:, ch].bitcast(FP8X4),
+                    lhsT_scale=c1_scales[:, ch],
+                    rhs=llc[:, px].bitcast(FP8X4),
+                    rhs_scale=lls[:, px],
+                    start=True,
+                    stop=True,
                 )
+            ybank_t[(b, h)] = bank
 
-        CENTER = 4
+        def bias1(b, h):
+            nc.vector.tensor_tensor(
+                out=y_bf[b][:, P * h : P * (h + 1), :],
+                in0=ybank_t[(b, h)][:].rearrange("p t n -> p n t"),
+                in1=b1[:].unsqueeze(1).to_broadcast([P, P, T]),
+                op=ALU.add,
+            )
+
+        def ybank_zk():
+            bank = pzk.tile([P, T, P], F32, name="ybank", tag="zk")
+            return bank
+
+        def ybank_sa():
+            bank = psa.tile([P, T, P], F32, name="ybank", tag="sa")
+            return bank
 
         def quant_y(b):
             nc.vector.quantize_mx(
@@ -211,31 +253,40 @@ def tile_merge_pa_kernel(tc, x, w_c1, b_c1, w_q, w_k, w_v_bytes, w_v_scale, bn_g
                 in_=y_bf[b][:].rearrange("p n j -> p (n j)"),
             )
 
-        def shift_codes(half):
+        def shift_codes(half, dj, eng):
             bs = slice(2 * half, 2 * half + 2)
             src = ys[0][:, bs, 16:272].bitcast(I32).rearrange("p b (i w) -> p b i w", w=16)
-            for dj in (-1, 1):
-                dst = ys[dj][:, bs, 16:272].bitcast(I32).rearrange("p b (i w) -> p b i w", w=16)
-                lo, hi = max(0, -dj), min(16, 16 - dj)
-                nc.vector.tensor_copy(out=dst[:, :, :, lo:hi], in_=src[:, :, :, lo + dj : hi + dj])
+            dst = ys[dj][:, bs, 16:272].bitcast(I32).rearrange("p b (i w) -> p b i w", w=16)
+            lo, hi = max(0, -dj), min(16, 16 - dj)
+            eng.tensor_copy(out=dst[:, :, :, lo:hi], in_=src[:, :, :, lo + dj : hi + dj])
 
-        def shift_scales(half):
+        def shift_scales_w(half, dj, eng):
             px = slice(512 * half, 512 * (half + 1))
+            lo, hi = max(0, -dj), min(16, 16 - dj)
+            dst = sp[:, CENTER + dj, px].rearrange("p (n w) -> p n w", w=16)
+            src = sp[:, CENTER, px].rearrange("p (n w) -> p n w", w=16)
+            eng.tensor_copy(out=dst[:, :, lo:hi], in_=src[:, :, lo + dj : hi + dj])
+
+        def shift_scales_h(half, dj, eng):
+            px = slice(512 * half, 512 * (half + 1))
+            src = sp[:, CENTER + dj, px].bitcast(I32).rearrange("p (b n) -> p b n", b=2)
+            for di in (-1, 1):
+                dst = sp[:, CENTER + 3 * di + dj, px].bitcast(I32).rearrange("p (b n) -> p b n", b=2)
+                lo, hi = max(0, -4 * di), min(64, 64 - 4 * di)
+                eng.tensor_copy(out=dst[:, :, lo:hi], in_=src[:, :, lo + 4 * di : hi + 4 * di])
+
+        def shifts(half, eng):
             for dj in (-1, 1):
-                lo, hi = max(0, -dj), min(16, 16 - dj)
-                dst = sp[:, 4 + dj, px].rearrange("p (n w) -> p n w", w=16)
-                src = sp[:, CENTER, px].rearrange("p (n w) -> p n w", w=16)
-                nc.vector.tensor_copy(out=dst[:, :, lo:hi], in_=src[:, :, lo + dj : hi + dj])
+                shift_scales_w(half, dj, eng)
+            for dj in (-1, 1):
+                shift_codes(half, dj, nc.vector)
             for dj in (-1, 0, 1):
-                src = sp[:, 4 + dj, px].bitcast(I32).rearrange("p (b n) -> p b n", b=2)
-                for di in (-1, 1):
-                    dst = sp[:, 4 + 3 * di + dj, px].bitcast(I32).rearrange("p (b n) -> p b n", b=2)
-                    lo, hi = max(0, -4 * di), min(64, 64 - 4 * di)
-                    nc.vector.tensor_copy(out=dst[:, :, lo:hi], in_=src[:, :, lo + 4 * di : hi + 4 * di])
+                shift_scales_h(half, dj, eng)
 
-        nq_t, qb_t, kb0_t, m_t, mparts = {}, {}, {}, {}, {}
+        qb_t, kb0_t, m_t, qt_t, mtt_t, ext_t = {}, {}, {}, {}, {}, {}
+        kbank_t, qbank_t, qtbank_t, mtbank_t, pr_t = {}, {}, {}, {}, {}
 
-        def qk_matmul(bank, codes, scales, ct, half):
+        def ch_matmuls(bank, codes, scales, ct, half):
             ch = slice(P * ct, P * (ct + 1))
             for bb in range(2):
                 b = 2 * half + bb
@@ -249,91 +300,7 @@ def tile_merge_pa_kernel(tc, x, w_c1, b_c1, w_q, w_k, w_v_bytes, w_v_scale, bn_g
                     stop=True,
                 )
 
-        def make_k(g):
-            ct, half = SB_ORDER[g]
-            bank = pzk.tile([P, HW], F32, name="kbank", tag="zk")
-            qk_matmul(bank, k_codes, k_scales, ct, half)
-            bv = bank[:].rearrange("p (b i w) -> p b i w", b=2, w=16)
-            nc.scalar.copy(out=kpad[g % 2][:, :, 1:17, 4:20], in_=bv)
-            kb0 = attn.tile([P, 2, 16, 16], BF16, name="kb0", tag="kb0", bufs=2)
-            kb0_t[g] = kb0
-            nc.scalar.copy(out=kb0[:].rearrange("p b i w -> p (b i w)"), in_=bank[:])
-            nc.scalar.copy(out=kb1[g % 2][:, :, :, 3:19], in_=kb0[:])
-
-        def make_q(g):
-            ct, half = SB_ORDER[g]
-            bank = pzk.tile([P, HW], F32, name="qbank", tag="zk")
-            qk_matmul(bank, q_codes, q_scales, ct, half)
-            nq = attn.tile([P, HW], F32, name="nq", tag="nq", bufs=2)
-            qb = attn.tile([P, HW], BF16, name="qb", tag="qb", bufs=2)
-            nq_t[g], qb_t[g] = nq, qb
-            nc.scalar.activation(out=nq[:], in_=bank[:], func=ACT.Copy, scale=-1.0)
-            nc.scalar.copy(out=qb[:], in_=bank[:])
-
-        def make_ext(g, which):
-            op = ALU.max if which == 0 else ALU.min
-            hx = (hmx if which == 0 else hmn)[g % 2]
-            k1 = kb1[g % 2]
-            tmp = attn.tile([P, 2, 16, 16], BF16, name="tmp", tag="tmp", bufs=2)
-            nc.vector.tensor_tensor(out=tmp[:], in0=k1[:, :, :, 2:18], in1=k1[:, :, :, 4:20], op=op)
-            nc.vector.tensor_tensor(out=hx[:, :, 1:17, :], in0=tmp[:], in1=kb0_t[g][:], op=op)
-            tmp2 = attn.tile([P, 2, 16, 16], BF16, name="tmp2", tag="tmp2", bufs=2)
-            nc.vector.tensor_tensor(out=tmp2[:], in0=hx[:, :, 0:16, :], in1=hx[:, :, 1:17, :], op=op)
-            ext = attn.tile([P, 2, 16, 16], BF16, name="ext", tag="ext%d" % which, bufs=2)
-            nc.vector.tensor_tensor(out=ext[:], in0=tmp2[:], in1=hx[:, :, 2:18, :], op=op)
-            mparts[(g, which)] = ext
-
-        def make_m(g):
-            prods = []
-            for which in range(2):
-                pr = attn.tile([P, HW], BF16, name="pr", tag="pr%d" % which, bufs=2)
-                nc.vector.tensor_tensor(
-                    out=pr[:], in0=qb_t[g][:], in1=mparts[(g, which)][:].rearrange("p b i w -> p (b i w)"), op=ALU.mult
-                )
-                prods.append(pr)
-            mt = attn.tile([P, HW], F32, name="mt", tag="mt", bufs=2)
-            nc.vector.tensor_tensor(out=mt[:], in0=prods[0][:], in1=prods[1][:], op=ALU.max)
-            m_t[g] = mt
-
-        NS = NOFF * len(SB_ORDER)
-        z_t, zm_t, e_t, v_t, ev_t, sa_t = {}, {}, {}, {}, {}, {}
-
-        def step_z(s):
-            g, j = divmod(s, NOFF)
-            di, dj = OFFSETS[j]
-            zt = attn.tile([P, HW], F32, name="zt", tag="zt")
-            z_t[s] = zt
-            eng = nc.vector if j in Z_ON_VECTOR else nc.gpsimd
-            eng.tensor_tensor(
-                out=zt[:].rearrange("p (b i w) -> p b i w", b=2, w=16),
-                in0=nq_t[g][:].rearrange("p (b i w) -> p b i w", b=2, w=16),
-                in1=kpad[g % 2][:, :, 1 + di : 17 + di, 4 + dj : 20 + dj],
-                op=ALU.mult,
-            )
-
-        def add_transposed(dst, src, start, stop):
-            nc.tensor.matmul(dst, lhsT=src, rhs=ident_f[:], start=start, stop=stop, is_transpose=True)
-
-        def step_zm(s):
-            g = s // NOFF
-            bank = pzk.tile([P, HW], F32, name="zmbank", tag="zk")
-            zm_t[s] = bank
-            for n in range(4):
-                blk = slice(P * n, P * (n + 1))
-                add_transposed(bank[:, blk], z_t[s][:, blk], True, False)
-                add_transposed(bank[:, blk], m_t[g][:, blk], False, True)
-
-        def step_exp(s):
-            et = attn.tile([P, HW], F32, name="et", tag="et")
-            e_t[s] = et
-            nc.scalar.activation(out=et[:], in_=zm_t[s][:], func=ACT.Exp, scale=-1.0)
-
-        def step_v(s):
-            g, j = divmod(s, NOFF)
-            ct, half = SB_ORDER[g]
-            di, dj = OFFSETS[j]
-            bank = pv.tile([P, HW], F32, name="vbank", tag="v")
-            v_t[s] = bank
+        def px_matmuls(bank, ct, half, di, dj, codes, scales):
             ch = slice(P * ct, P * (ct + 1))
             for n in range(4):
                 b, r0 = 2 * half + n // 2, 8 * (n % 2)
@@ -342,15 +309,144 @@ def tile_merge_pa_kernel(tc, x, w_c1, b_c1, w_q, w_k, w_v_bytes, w_v_scale, bn_g
                 nc.tensor.matmul_mx(
                     out=bank[:, P * n : P * (n + 1)],
                     lhsT=ys[dj][:, b, w0 : w0 + P].bitcast(FP8X4),
-                    lhsT_scale=sp[:, 4 + 3 * di + dj, px : px + P],
-                    rhs=v_codes[:, ch].bitcast(FP8X4),
-                    rhs_scale=v_scales[:, ch],
+                    lhsT_scale=sp[:, CENTER + 3 * di + dj, px : px + P],
+                    rhs=codes[:, ch].bitcast(FP8X4),
+                    rhs_scale=scales[:, ch],
                     start=True,
                     stop=True,
                 )
 
+        def make_k(g):
+            ct, half = SB_ORDER[g]
+            bank = pzk.tile([P, HW], F32, name="kbank", tag="zk")
+            ch_matmuls(bank, k_codes, k_scales, ct, half)
+            kbank_t[g] = bank
+
+        def copy_k(g):
+            bank = kbank_t[g]
+            kb0 = attn.tile([P, 2, 16, 16], BF16, name="kb0", tag="kb0")
+            kb0_t[g] = kb0
+            nc.scalar.copy(out=kb0[:].rearrange("p b i w -> p (b i w)"), in_=bank[:])
+            nc.scalar.copy(out=kb1[g % 2][:, :, :, 3:19], in_=kb0[:])
+
+        def make_q(g):
+            ct, half = SB_ORDER[g]
+            bank = pzk.tile([P, HW], F32, name="qbank", tag="zk")
+            ch_matmuls(bank, q_codes, q_scales, ct, half)
+            qbank_t[g] = bank
+
+        def copy_q(g):
+            bank = qbank_t[g]
+            qb = attn.tile([P, HW], BF16, name="qb", tag="qb")
+            qb_t[g] = qb
+            nc.scalar.copy(out=qb[:], in_=bank[:])
+
+        def make_qt(g):
+            ct, half = SB_ORDER[g]
+            bank = pzk.tile([P, HW], F32, name="qtbank", tag="zk")
+            px_matmuls(bank, ct, half, 0, 0, q_codes, q_scales)
+            qtbank_t[g] = bank
+
+        def copy_qt(g):
+            bank = qtbank_t[g]
+            qt = attn.tile([P, HW], F32, name="qt", tag="qt")
+            qt_t[g] = qt
+            nc.scalar.copy(out=qt[:], in_=bank[:])
+
+        def make_ext(g, stage):
+            k1, k0 = kb1[g % 2], kb0_t[g]
+            for which, op in enumerate((ALU.max, ALU.min)):
+                hx = (hmx, hmn)[which][g % 2]
+                if stage == 0:
+                    tmp = attn.tile([P, 2, 16, 16], BF16, name="tmp", tag="tmp%d" % which, bufs=1)
+                    nc.vector.tensor_tensor(out=tmp[:], in0=k1[:, :, :, 2:18], in1=k1[:, :, :, 4:20], op=op)
+                    ext_t[which] = tmp
+                elif stage == 1:
+                    nc.vector.tensor_tensor(out=hx[:, :, 1:17, :], in0=ext_t[which][:], in1=k0[:], op=op)
+                elif stage == 2:
+                    pair = attn.tile([P, 2, 8, 16], BF16, name="pair", tag="pair%d" % which, bufs=1)
+                    hp = hx[:, :, 1:17, :].rearrange("p b (i r) w -> p b i r w", r=2)
+                    nc.vector.tensor_tensor(out=pair[:], in0=hp[:, :, :, 0, :], in1=hp[:, :, :, 1, :], op=op)
+                    ext_t[which] = pair
+                else:
+                    pair = ext_t[which]
+                    ext = attn.tile([P, 2, 16, 16], BF16, name="ext", tag="ext%d" % which, bufs=1)
+                    ev_ = ext[:].rearrange("p b (i r) w -> p b i r w", r=2)
+                    nc.vector.tensor_tensor(out=ev_[:, :, :, 0, :], in0=pair[:], in1=hx[:, :, 0:16:2, :], op=op)
+                    nc.vector.tensor_tensor(out=ev_[:, :, :, 1, :], in0=pair[:], in1=hx[:, :, 3:18:2, :], op=op)
+                    ext_t[(g, which)] = ext
+
+        def make_prod(g, which):
+            pr = attn.tile([P, HW], BF16, name="pr", tag="pr%d" % which, bufs=1)
+            nc.vector.tensor_tensor(
+                out=pr[:], in0=qb_t[g][:], in1=ext_t[(g, which)][:].rearrange("p b i w -> p (b i w)"), op=ALU.mult
+            )
+            pr_t[(g, which)] = pr
+
+        def make_m(g):
+            mt = attn.tile([P, HW], F32, name="mt", tag="mt", bufs=1)
+            nc.vector.tensor_tensor(out=mt[:], in0=pr_t[(g, 0)][:], in1=pr_t[(g, 1)][:], op=ALU.max)
+            m_t[g] = mt
+
+        def make_mt(g):
+            bank = pzk.tile([P, HW], F32, name="mtbank", tag="zk")
+            for n in range(4):
+                blk = slice(P * n, P * (n + 1))
+                nc.tensor.transpose(bank[:, blk], m_t[g][:, blk], ident_f[:])
+            mtbank_t[g] = bank
+
+        def copy_mt(g):
+            bank = mtbank_t[g]
+            mtt = attn.tile([P, HW], F32, name="mtt", tag="mtt")
+            mtt_t[g] = mtt
+            nc.scalar.copy(out=mtt[:], in_=bank[:])
+
+        NS = NOFF * len(SB_ORDER)
+        kt_t, zd_t, z_t, e_t, v_t, ev_t, sa_t = {}, {}, {}, {}, {}, {}, {}
+
+        def step_kt(s):
+            g, j = divmod(s, NOFF)
+            bank = pzk.tile([P, HW], F32, name="ktbank", tag="zk")
+            px_matmuls(bank, *SB_ORDER[g], *OFFSETS[j], k_codes, k_scales)
+            kt_t[s] = bank
+
+        def step_v(s):
+            g, j = divmod(s, NOFF)
+            bank = pv.tile([P, HW], F32, name="vbank", tag="v")
+            v_t[s] = bank
+            keeper(s)
+            px_matmuls(bank, *SB_ORDER[g], *OFFSETS[j], v_codes, v_scales)
+
+        def keeper(s):
+            if KEEP:
+                nc.tensor.matmul_mx(
+                    out=v_t[s][:, 0:KEEP],
+                    lhsT=k_codes[:, 0:P].bitcast(FP8X4),
+                    lhsT_scale=k_scales[:, 0:P],
+                    rhs=k_codes[:, 0:KEEP].bitcast(FP8X4),
+                    rhs_scale=k_scales[:, 0:KEEP],
+                    start=True,
+                    stop=True,
+                )
+
+        def step_qk(s):
+            zd = attn.tile([P, HW], F32, name="zd", tag="zd", bufs=7)
+            zd_t[s] = zd
+            nc.vector.tensor_tensor(out=zd[:], in0=kt_t[s][:], in1=qt_t[s // NOFF][:], op=ALU.mult)
+
+        def step_z(s):
+            zt = attn.tile([P, HW], F32, name="zt", tag="zt", bufs=4)
+            z_t[s] = zt
+            eng = nc.vector if s % NOFF in V_SUB else nc.gpsimd
+            eng.tensor_tensor(out=zt[:], in0=zd_t[s][:], in1=mtt_t[s // NOFF][:], op=ALU.subtract)
+
+        def step_exp(s):
+            et = attn.tile([P, HW], F32, name="et", tag="et", bufs=5)
+            e_t[s] = et
+            nc.scalar.activation(out=et[:], in_=z_t[s][:], func=ACT.Exp)
+
         def step_ev(s):
-            evt = attn.tile([P, HW], F32, name="evt", tag="evt")
+            evt = attn.tile([P, HW], F32, name="evt", tag="evt", bufs=3)
             ev_t[s] = evt
             nc.vector.tensor_tensor(out=evt[:], in0=v_t[s][:], in1=e_t[s][:], op=ALU.mult)
 
@@ -363,163 +459,256 @@ def tile_merge_pa_kernel(tc, x, w_c1, b_c1, w_q, w_k, w_v_bytes, w_v_scale, bn_g
             for bank, src in zip(sa_t[g], (e_t[s], ev_t[s])):
                 for n in range(4):
                     blk = slice(P * n, P * (n + 1))
-                    add_transposed(bank[:, blk], src[:, blk], j == 0 and n == 0, j == NOFF - 1 and n == 3)
+                    nc.tensor.matmul(
+                        bank[:, blk],
+                        lhsT=src[:, blk],
+                        rhs=ident_f[:],
+                        start=(j == 0 and n == 0),
+                        stop=(j == NOFF - 1 and n == 3),
+                        is_transpose=True,
+                    )
 
-        ss_t, as_t, r_t, att_t, aff_t = {}, {}, {}, {}, {}
-        small = {}
+        jobs = {}
+
+        def at_slot(i, kind, fn, *args):
+            jobs.setdefault((i, kind), []).append((fn, args))
+
+        def run(i, kind):
+            for fn, args in jobs.get((i, kind), []):
+                fn(*args)
+
+        def pipeline(i):
+            if 0 <= i + L_K < NS:
+                step_kt(i + L_K)
+            run(i, "mx")
+            if 0 <= i + L_V < NS:
+                step_v(i + L_V)
+            run(i, "a")
+            if 0 <= i + L_X < NS:
+                step_exp(i + L_X)
+            if 0 <= i + L_EV < NS:
+                step_ev(i + L_EV)
+            if 0 <= i + L_K < NS:
+                step_qk(i + L_K)
+            run(i, "v")
+            if 0 <= i + L_Z < NS:
+                step_z(i + L_Z)
+            run(i, "g")
+            if 0 <= i < NS:
+                step_sa(i)
+            run(i, "tr")
+            run(i, "a2")
+
+        ss_t, at_t, r_t, cs_t, bn_t, rs_t, re_t, li_t = {}, {}, {}, {}, {}, {}, {}, {}
 
         def sums_out(g):
             ct, half = SB_ORDER[g]
             if ct not in ss_t:
                 ss = attn.tile([P, 1024], F32, name="ss", tag="ss", bufs=3)
-                as_ = attn.tile([P, 1024], F32, name="as_", tag="as", bufs=3)
-                ss_t[ct], as_t[ct] = ss, as_
+                at = attn.tile([P, 1024], F32, name="at", tag="at", bufs=3)
+                ss_t[ct], at_t[ct] = ss, at
             sl = slice(HW * half, HW * (half + 1))
             nc.scalar.copy(out=ss_t[ct][:, sl], in_=sa_t[g][0][:])
-            nc.scalar.copy(out=as_t[ct][:, sl], in_=sa_t[g][1][:])
+            nc.scalar.copy(out=at_t[ct][:, sl], in_=sa_t[g][1][:])
 
         def recip(ct):
-            ln = attn.tile([P, 1024], F32, name="ln", tag="ln", bufs=1)
+            ln = attn.tile([P, 1024], F32, name="ln", tag="ln")
             nc.scalar.activation(out=ln[:], in_=ss_t[ct][:], func=ACT.Ln)
-            r = attn.tile([P, 1024], F32, name="r", tag="r", bufs=1)
-            nc.scalar.activation(out=r[:], in_=ln[:], func=ACT.Exp, scale=-1.0)
-            r_t[ct] = r
+            nc.scalar.activation(out=ln[:], in_=ln[:], func=ACT.Exp, scale=-1.0)
+            r_t[ct] = ln
 
-        def normalise(ct):
-            at = attn.tile([P, 1024], F32, name="at", tag="at", bufs=2)
-            att_t[ct] = at
-            stats = attn.tile([P, 2, 6], F32, name="stats", tag="stats", bufs=2)
-            for h in range(2):
-                sl = slice(HW * h, HW * (h + 1))
-                nc.vector.tensor_tensor(out=at[:, sl], in0=as_t[ct][:, sl], in1=r_t[ct][:, sl], op=ALU.mult)
-            for h in range(2):
-                nc.vector.bn_stats(out=stats[:, h, :], in_=at[:, HW * h : HW * (h + 1)])
-            mv = attn.tile([P, 2], F32, name="mv", tag="mv", bufs=2)
-            nc.vector.bn_aggr(out=mv[:], in_=stats[:].rearrange("p h s -> p (h s)"))
-            small[ct] = mv
+        def attend(ct, h):
+            at = at_t[ct]
+            if h == 0:
+                bn = attn.tile([P, 8], F32, name="bn", tag="bn")
+                bn_t[ct] = bn
+            sl = slice(HW * h, HW * (h + 1))
+            nc.vector.scalar_tensor_tensor(
+                out=at[:, sl], in0=at[:, sl], scalar=1.0, in1=r_t[ct][:, sl], op0=ALU.mult, op1=ALU.mult,
+                accum_out=bn_t[ct][:, h : h + 1],
+            )
 
-        gam = keep.tile([P, T], F32, name="gam")
+        def negmean(ct):
+            bn = bn_t[ct]
+            nc.vector.tensor_scalar(
+                out=bn[:, 2:3], in0=bn[:, 0:1], scalar1=bn[:, 1:2], scalar2=-1.0 / 1024, op0=ALU.add, op1=ALU.mult
+            )
+
+        def squares(ct):
+            bn = bn_t[ct]
+            nc.scalar.activation(
+                out=r_t[ct][:], in_=at_t[ct][:], func=ACT.Square, bias=bn[:, 2:3], accum_out=bn[:, 3:4]
+            )
+
+        gam = keep.tile([P, T, 2], F32, name="gam")
         bet = keep.tile([P, T], F32, name="bet")
         aa = keep.tile([P, 1], F32, name="aa")
         oma = keep.tile([P, 1], F32, name="oma")
 
+        def load_affine():
+            nc.vector.tensor_copy(out=aa[:], in_=a_b[:])
+            nc.vector.tensor_copy(out=bet[:], in_=bet_b[:])
+            nc.vector.tensor_copy(out=gam[:, :, 0], in_=gam_b[:])
+            nc.vector.tensor_scalar(out=gam[:, :, 1], in0=gam[:, :, 0], scalar1=aa[:], scalar2=None, op0=ALU.mult)
+            nc.vector.tensor_scalar(out=oma[:], in0=aa[:], scalar1=-1.0, scalar2=1.0, op0=ALU.mult, op1=ALU.add)
+
         def affine(ct):
-            mv = small[ct]
-            cs = attn.tile([P, 8], F32, name="cs", tag="cs", bufs=2)
-            aff_t[ct] = cs
-            g_ = nc.gpsimd
-            g_.tensor_scalar(out=cs[:, 0:1], in0=mv[:, 1:2], scalar1=1.0, scalar2=1e-5, op0=ALU.mult, op1=ALU.add)
-            g_.tensor_tensor(out=cs[:, 1:2], in0=cs[:, 0:1], in1=neghalf[:], op=ALU.pow)
-            g_.tensor_tensor(out=cs[:, 2:3], in0=cs[:, 1:2], in1=gam[:, ct : ct + 1], op=ALU.mult)
-            g_.tensor_tensor(out=cs[:, 3:4], in0=cs[:, 2:3], in1=mv[:, 0:1], op=ALU.mult)
-            g_.tensor_tensor(out=cs[:, 4:5], in0=bet[:, ct : ct + 1], in1=cs[:, 3:4], op=ALU.subtract)
-            g_.tensor_tensor(out=cs[:, 5:6], in0=cs[:, 2:3], in1=aa[:], op=ALU.mult)
-            g_.tensor_tensor(out=cs[:, 6:7], in0=cs[:, 4:5], in1=aa[:], op=ALU.mult)
+            bn = bn_t[ct]
+            rs = attn.tile([P, 2], F32, name="rs", tag="rs")
+            rs_t[ct] = rs
+            nc.gpsimd.tensor_scalar(
+                out=rs[:, 0:1], in0=bn[:, 3:4], scalar1=1.0 / 1024, scalar2=1e-5, op0=ALU.mult, op1=ALU.add
+            )
+            nc.gpsimd.tensor_tensor(out=rs[:, 1:2], in0=rs[:, 0:1], in1=neghalf[:], op=ALU.pow)
+
+        def affine2(ct):
+            bn, rs = bn_t[ct], rs_t[ct]
+            cs = attn.tile([P, 8], F32, name="cs", tag="cs")
+            cs_t[ct] = cs
+            nc.vector.tensor_scalar(out=cs[:, 0:2], in0=gam[:, ct, :], scalar1=rs[:, 1:2], scalar2=None, op0=ALU.mult)
+            nc.vector.scalar_tensor_tensor(
+                out=cs[:, 2:3], in0=bn[:, 2:3], scalar=cs[:, 0:1], in1=bet[:, ct : ct + 1], op0=ALU.mult, op1=ALU.add
+            )
+            nc.vector.tensor_scalar(out=cs[:, 3:4], in0=cs[:, 2:3], scalar1=aa[:], scalar2=None, op0=ALU.mult)
 
         out_v = out.rearrange("b (p t) h w -> t p b (h w)", t=T)
 
-        def finish(ct):
-            cs, at = aff_t[ct], att_t[ct]
-            for h in range(2):
-                sl = slice(HW * h, HW * (h + 1))
-                re = attn.tile([P, HW], F32, name="re", tag="re", bufs=2)
-                li = attn.tile([P, HW], F32, name="li", tag="li", bufs=2)
-                res = attn.tile([P, HW], F32, name="res", tag="res", bufs=2)
-                nc.scalar.activation(out=re[:], in_=at[:, sl], func=ACT.Relu, scale=cs[:, 2:3], bias=cs[:, 4:5])
-                nc.scalar.activation(out=li[:], in_=at[:, sl], func=ACT.Identity, scale=cs[:, 5:6], bias=cs[:, 6:7])
-                nc.vector.scalar_tensor_tensor(
-                    out=res[:], in0=re[:], scalar=oma[:], in1=li[:], op0=ALU.mult, op1=ALU.add
+        def finish(ct, h):
+            cs, at = cs_t[ct], at_t[ct]
+            sl = slice(HW * h, HW * (h + 1))
+            re = attn.tile([P, HW], F32, name="re", tag="re")
+            li = attn.tile([P, HW], F32, name="li", tag="li")
+            re_t[(ct, h)], li_t[(ct, h)] = re, li
+            nc.scalar.activation(out=re[:], in_=at[:, sl], func=ACT.Relu, scale=cs[:, 0:1], bias=cs[:, 2:3])
+            if ct == 3 or LI_V:
+                nc.vector.tensor_scalar(
+                    out=li[:], in0=at[:, sl], scalar1=cs[:, 1:2], scalar2=cs[:, 3:4], op0=ALU.mult, op1=ALU.add
                 )
-                nc.sync.dma_start(
-                    out=out_v[ct][:, 2 * h : 2 * h + 2, :], in_=res[:].rearrange("p (b n) -> p b n", b=2)
-                )
+            else:
+                nc.scalar.activation(out=li[:], in_=at[:, sl], func=ACT.Identity, scale=cs[:, 1:2], bias=cs[:, 3:4])
 
-        haar_pe(0)
+        def finish2(ct, h):
+            re, li = re_t[(ct, h)], li_t[(ct, h)]
+            nc.vector.scalar_tensor_tensor(out=re[:], in0=re[:], scalar=oma[:], in1=li[:], op0=ALU.mult, op1=ALU.add)
+            nc.sync.dma_start(out=out_v[ct][:, 2 * h : 2 * h + 2, :], in_=re[:].rearrange("p (b n) -> p b n", b=2))
+
+        vcopy = nc.vector.tensor_copy
+        acopy = nc.scalar.copy
+        haar_alloc(0)
         haar_alloc(1)
-        haar_part(1, nc.gpsimd, 2, 4)
-        haar_part(1, nc.vector, 0, 2)
-        c1_codes, c1_scales = prep_weight(as_words(raw_c1), "c1", nc.scalar.copy)
+        c1_tr = tr_weight(as_words(raw_c1), "c1", psa, "sa")
+        haar_pe(1, 0)
+        k_tr = tr_weight(as_words(raw_k), "wk", pv, "v")
+        q_tr = tr_weight(as_words(raw_q), "wq", psa, "sa")
+        copy_weight(c1_tr, (acopy, vcopy))
+        haar_v(0, 0, 0, 2)
+        haar_v(0, 0, 2, 4)
+        haar_v(0, 1)
+        c1_codes, c1_scales = quant_weight(c1_tr)
+        haar_v(1, 1)
+        haar_group(0, 0)
+        haar_group(0, 1)
+        haar_pe_out(1, 0)
+        haar_group(1, 1)
         quant_ll(0)
-        haar_group(1)
-        conv1(0)
-        k_codes, k_scales = prep_weight(as_words(raw_k), "wk", nc.scalar.copy)
-        quant_y(0)
-        quant_ll(1)
-        conv1(1)
-        q_codes, q_scales = prep_weight(as_words(raw_q), "wq", nc.scalar.copy)
-        quant_y(1)
-        make_k(0)
-        make_q(0)
-        make_ext(0, 0)
-        make_ext(0, 1)
-        make_m(0)
-        step_z(0)
-        step_z(1)
-        step_z(2)
         wv_bf = raws.tile([P, T, 512], BF16, name="wv_bf")
-        for t in range(T):
+
+        def wv_product(t):
             nc.vector.tensor_tensor(out=wv_bf[:, t, :], in0=raw_vb[:, t, :].bitcast(FP8), in1=vscale[:], op=ALU.mult)
-        v_codes, v_scales = prep_weight(as_words(wv_bf), "wv", nc.scalar.copy)
-        shift_codes(0)
-        shift_scales(0)
-        nc.vector.tensor_copy(out=gam[:], in_=gam_b[:])
-        nc.vector.tensor_copy(out=bet[:], in_=bet_b[:])
-        nc.vector.tensor_copy(out=aa[:], in_=a_b[:])
-        nc.vector.tensor_scalar(out=oma[:], in0=aa[:], scalar1=-1.0, scalar2=1.0, op0=ALU.mult, op1=ALU.add)
-        step_zm(0)
-        step_exp(0)
-        step_v(0)
-        step_zm(1)
-        step_exp(1)
-        step_v(1)
-        step_ev(0)
 
-        extras = {}
-
-        def at_slot(i, fn, *args):
-            extras.setdefault(i, []).append((fn, args))
-
-        for n, b in enumerate((2, 3)):
-            base = 7 * n
-            at_slot(base, haar_alloc, b)
-            for t in range(T):
-                at_slot(base + t, haar_part, b, nc.vector, t, t + 1)
-            at_slot(base + 4, haar_group, b)
-            at_slot(base + 5, quant_ll, b)
-            at_slot(base + 5, conv1, b)
-            at_slot(base + 6, quant_y, b)
-        at_slot(15, shift_codes, 1)
-        at_slot(15, shift_scales, 1)
+        wv_product(0)
+        quant_ll(1)
+        copy_weight(k_tr, (acopy, acopy))
+        for b in range(2):
+            for h in range(2):
+                conv1(b, h, ybank_zk())
+        bias1(0, 0)
+        bias1(0, 1)
+        quant_y(0)
+        bias1(1, 0)
+        bias1(1, 1)
+        quant_y(1)
+        k_codes, k_scales = quant_weight(k_tr)
+        copy_weight(q_tr, (acopy, acopy))
+        for t in range(1, T):
+            wv_product(t)
+        make_k(0)
+        copy_k(0)
+        q_codes, q_scales = quant_weight(q_tr)
+        make_q(0)
+        copy_q(0)
+        make_qt(0)
+        v_tr = tr_weight(as_words(wv_bf), "wv", psa, "sa")
+        copy_qt(0)
+        for stage in range(4):
+            make_ext(0, stage)
+        make_prod(0, 0)
+        make_prod(0, 1)
+        make_m(0)
+        make_mt(0)
+        copy_weight(v_tr, (acopy, vcopy))
+        copy_mt(0)
+        shift_scales_h(0, 0, nc.vector)
+        for dj in (1, -1):
+            shift_scales_w(0, dj, nc.vector)
+        v_codes, v_scales = quant_weight(v_tr)
+        for dj in (1, -1):
+            shift_codes(0, dj, nc.vector)
+            shift_scales_h(0, dj, nc.vector)
+        for b in (2, 3):
+            s = 6 * (b - 2)
+            at_slot(s, "mx", haar_alloc, b)
+            for h in range(2):
+                if 2 * (b - 2) + h + 1 < N_PE_HAAR:
+                    at_slot(s + h, "mx", haar_pe, b, h)
+                    at_slot(s + h + 1, "a", haar_pe_out, b, h)
+                else:
+                    at_slot(s + h, "v", haar_v, b, h)
+                    at_slot(s + h + 1, "a", haar_group, b, h)
+            at_slot(s + 3, "v", quant_ll, b)
+            for h in range(2):
+                at_slot(s + 4 + h, "mx", lambda b_, h_: conv1(b_, h_, ybank_zk()), b, h)
+                at_slot(s + 5 + h, "v", bias1, b, h)
+            at_slot(s + 7, "v", quant_y, b)
+        for dj in (-1, 1):
+            at_slot(14, "v", shift_scales_w, 1, dj, nc.vector)
+            at_slot(14, "v", shift_codes, 1, dj, nc.vector)
+        for dj in (-1, 0, 1):
+            at_slot(15, "v", shift_scales_h, 1, dj, nc.vector)
+        at_slot(16, "v", load_affine)
 
         done = set()
         for g, (ct, half) in enumerate(SB_ORDER):
             s0 = NOFF * g
-            if g + 1 < len(SB_ORDER):
-                at_slot(s0 + 0, make_k, g + 1)
-                at_slot(s0 + 1, make_q, g + 1)
-                at_slot(s0 + 3, make_ext, g + 1, 0)
-                at_slot(s0 + 4, make_ext, g + 1, 1)
-                at_slot(s0 + 5, make_m, g + 1)
+            if g > 0:
+                at_slot(max(0, s0 + E_K), "mx", make_k, g)
+                at_slot(max(0, s0 + E_K), "a", copy_k, g)
+                at_slot(max(0, s0 + E_QT), "mx", make_qt, g)
+                at_slot(max(0, s0 + E_QT), "a", copy_qt, g)
+                at_slot(max(0, s0 + E_Q), "mx", make_q, g)
+                at_slot(max(0, s0 + E_Q), "a", copy_q, g)
+                for n in range(4):
+                    at_slot(max(0, s0 + E_CH), "v", make_ext, g, n)
+                at_slot(max(0, s0 + E_CH), "v", make_prod, g, 0)
+                at_slot(max(0, s0 + E_CH), "v", make_prod, g, 1)
+                at_slot(max(0, s0 + E_CH), "v", make_m, g)
+                at_slot(max(0, s0 + E_MT), "tr", make_mt, g)
+                at_slot(max(0, s0 + E_MT), "a2", copy_mt, g)
             e0 = s0 + NOFF
-            at_slot(e0, sums_out, g)
+            at_slot(e0, "a", sums_out, g)
             if ct in done:
-                at_slot(e0 + 1, recip, ct)
-                at_slot(e0 + 2, normalise, ct)
-                at_slot(e0 + 3, affine, ct)
-                at_slot(e0 + 4, finish, ct)
+                f = (lambda n, e0=e0: e0 + n)
+                at_slot(f(F_LN), "a", recip, ct)
+                at_slot(f(F_A), "v", attend, ct, 0)
+                at_slot(f(F_A), "v", attend, ct, 1)
+                at_slot(f(F_A), "v", negmean, ct)
+                at_slot(f(F_SQ), "a", squares, ct)
+                at_slot(f(F_RS), "g", affine, ct)
+                at_slot(f(F_CS), "v", affine2, ct)
+                at_slot(f(F_R), "a", finish, ct, 0)
+                at_slot(f(F_R + 1), "a", finish, ct, 1)
+                at_slot(f(F_O), "v", finish2, ct, 0)
+                at_slot(f(F_O), "v", finish2, ct, 1)
             done.add(ct)
-
-        for i in range(NS + NOFF):
-            if i + 2 < NS:
-                step_zm(i + 2)
-                step_exp(i + 2)
-            if i + 3 < NS:
-                step_z(i + 3)
-            if i + 1 < NS:
-                step_ev(i + 1)
-            if i < NS:
-                step_sa(i)
-            if i + 2 < NS:
-                step_v(i + 2)
-            for fn, args in extras.get(i, []):
-                fn(*args)
+        for i in range(-L_K, NS + 25):
+            pipeline(i)

from contextlib import ExitStack

import concourse.mybir as mybir
from concourse.masks import make_identity

B, C, M, O = 4, 512, 512, 512
NPX = 256
P = 128
T = 4
HW = 512
FLOPS = 2 * B * NPX * C * M * 4 + B * O * NPX * 9 * 6

F32 = mybir.dt.float32
BF16 = mybir.dt.bfloat16
U32 = mybir.dt.uint32
I32 = mybir.dt.int32
U8 = mybir.dt.uint8
FP8 = mybir.dt.float8_e4m3fn
FP8X4 = mybir.dt.float8_e4m3fn_x4
ALU = mybir.AluOpType
ACT = mybir.ActivationFunctionType

OFFSETS = [(di, dj) for dj in (0, 1, -1) for di in (0, 1, -1)]
NOFF = 9
CENTER = 4
SB_ORDER = [(0, 0), (1, 0), (2, 0), (0, 1), (1, 1), (2, 1), (3, 0), (3, 1)]
L_X = 3
L_Z = 5
L_K = 6
L_EV = 1
L_V = 2
E_K = -13
E_QT = -12
E_Q = -10
E_CH = -10
E_MT = -6
F_LN = 2
F_A = 3
F_SQ = 7
F_RS = 7
F_CS = 9
F_R = 12
F_O = 14
V_SUB = (5,)
KEEP = 0
LI_V = 0
B_ZK = 3
B_V = 3
B_SA = 2
N_PE_HAAR = 3


def tile_merge_pa_kernel(tc, x, w_c1, b_c1, w_q, w_k, w_v_bytes, w_v_scale, bn_gamma, bn_beta, prelu_a, out):
    nc = tc.nc
    with ExitStack() as ctx:
        keep = ctx.enter_context(tc.tile_pool(name="keep", bufs=1))
        raws = ctx.enter_context(tc.tile_pool(name="raws", bufs=1))
        work = ctx.enter_context(tc.tile_pool(name="work", bufs=2))
        attn = ctx.enter_context(tc.tile_pool(name="attn", bufs=2))
        pzk = ctx.enter_context(tc.psum_pool(name="pzk", bufs=B_ZK))
        pv = ctx.enter_context(tc.psum_pool(name="pv", bufs=B_V))
        psa = ctx.enter_context(tc.psum_pool(name="psa", bufs=B_SA))
        ctx.enter_context(tc.manual_schedule())

        xs = []
        for b in range(B):
            xb = raws.tile([P, T, 1024], BF16, name="x%d" % b)
            xs.append(xb)

        def load_x(b):
            view = x[b].rearrange("(p t) h w -> p t (h w)", t=T)
            for tt in range(2):
                nc.sync.dma_start(out=xs[b][:, 2 * tt : 2 * tt + 2, :], in_=view[:, 2 * tt : 2 * tt + 2, :])

        def load_w(ap, name):
            raw = raws.tile([P, T, 512], BF16, name=name)
            nc.sync.dma_start(out=raw[:], in_=ap.rearrange("(p t) k -> p t k", t=T))
            return raw

        raw_c1 = load_w(w_c1, "raw_c1")
        load_x(0)
        load_x(1)
        b1 = keep.tile([P, T], BF16, name="b1")
        nc.sync.dma_start(out=b1[:], in_=b_c1.rearrange("(p t) -> p t", t=T))
        raw_k = load_w(w_k, "raw_k")
        raw_q = load_w(w_q, "raw_q")
        raw_vb = raws.tile([P, T, 512], U8, name="raw_vb")
        nc.sync.dma_start(out=raw_vb[:], in_=w_v_bytes.rearrange("(p t) k -> p t k", t=T))
        vscale = raws.tile([P, 512], F32, name="vscale")
        nc.sync.dma_start(out=vscale[:], in_=w_v_scale.rearrange("o k -> (o k)").partition_broadcast(P))
        load_x(2)
        load_x(3)
        gam_b = keep.tile([P, T], BF16, name="gam_b")
        bet_b = keep.tile([P, T], BF16, name="bet_b")
        a_b = keep.tile([P, 1], BF16, name="a_b")
        nc.sync.dma_start(out=gam_b[:], in_=bn_gamma.rearrange("(p t) -> p t", t=T))
        nc.sync.dma_start(out=bet_b[:], in_=bn_beta.rearrange("(p t) -> p t", t=T))
        nc.sync.dma_start(out=a_b[:], in_=prelu_a.partition_broadcast(P))

        ident_f = keep.tile([P, P], F32, name="ident_f")
        make_identity(nc, ident_f[:])
        ident_b = keep.tile([P, P], BF16, name="ident_b")
        make_identity(nc, ident_b[:])
        kb1, hmx, hmn = [], [], []
        for par in range(2):
            kb_t = keep.tile([P, 2, 16, 20], BF16, name="kb1_%d" % par)
            nc.gpsimd.memset(kb_t[:].rearrange("p b i w -> p (b i w)").bitcast(I32), 0)
            kb1.append(kb_t)
            for lst, nm in ((hmx, "hmx"), (hmn, "hmn")):
                h_t = keep.tile([P, 2, 18, 16], BF16, name="%s%d" % (nm, par))
                nc.gpsimd.memset(h_t[:].rearrange("p b i w -> p (b i w)").bitcast(I32), 0)
                lst.append(h_t)
        sp = keep.tile([P, NOFF, 1024], U8, name="sp", align_bytes=64)
        nc.gpsimd.memset(sp[:].rearrange("p o n -> p (o n)").bitcast(I32), 0)
        ys = {}
        for dj in (0, -1, 1):
            y_t = keep.tile([P, B, 288], U32, name="ys%d" % (dj + 1), align_bytes=64)
            nc.gpsimd.memset(y_t[:].rearrange("p b n -> p (b n)").bitcast(I32), 0)
            ys[dj] = y_t
        neghalf = keep.tile([P, 1], F32, name="neghalf")
        nc.gpsimd.memset(neghalf[:], -0.5)

        def tr_weight(words, name, pool, tag):
            banks = []
            for half in range(2):
                bank = pool.tile([P, 2, 2, P], F32, name="wbank", tag=tag)
                for tt in range(2):
                    t = 2 * half + tt
                    for u in range(2):
                        nc.tensor.transpose(bank[:, tt, u, :], words[:, 256 * t + u : 256 * (t + 1) : 2], ident_f[:])
                banks.append(bank)
            grouped = work.tile([P, 512, 4], BF16, name="grouped", align_bytes=64)
            return name, banks, grouped

        def copy_weight(w, copies):
            gw = w[2][:].rearrange("p n j -> p (n j)").bitcast(F32)
            for half in range(2):
                copies[half](
                    out=gw[:, 512 * half : 512 * (half + 1)].rearrange("p (t r u) -> p t r u", t=2, u=2),
                    in_=w[1][half][:].rearrange("p t u r -> p t r u"),
                )

        def quant_weight(w):
            codes = keep.tile([P, 512], U32, name=w[0] + "_codes", align_bytes=64)
            scales = keep.tile([P, 512], U8, name=w[0] + "_scales", align_bytes=64)
            nc.vector.quantize_mx(out=codes[:].bitcast(FP8X4), scales=scales[:], in_=w[2][:].rearrange("p n j -> p (n j)"))
            return codes, scales

        def as_words(raw):
            return raw[:].rearrange("p t k -> p (t k)").bitcast(F32)

        llc = keep.tile([P, 1024], U32, name="llc", align_bytes=64)
        lls = keep.tile([P, 1024], U8, name="lls", align_bytes=64)
        ll_bf, haar_tiles, hbank_t = {}, {}, {}

        def haar_alloc(b):
            lb = work.tile([P, NPX, 4], BF16, name="ll_bf", tag="ll_bf", align_bytes=64)
            ll_bf[b] = lb
            hr = work.tile([P, 64, 32], F32, name="hr", tag="hr", bufs=1)
            lo = work.tile([P, 64, 16], F32, name="lo", tag="lo", bufs=2)
            haar_tiles[b] = (hr, lo)

        def haar_pe(b, h):
            bank = pzk.tile([P, T, P], F32, name="hbank", tag="zk")
            for t in range(T):
                view = xs[b][:, t, :].rearrange("p (i r w c) -> p i r w c", r=2, w=16, c=2)
                for n, (r, c) in enumerate(((0, 0), (0, 1), (1, 0), (1, 1))):
                    nc.tensor.matmul(
                        bank[:, t, :].rearrange("p (i w) -> p i w", w=16),
                        lhsT=ident_b[:],
                        rhs=view[:, 8 * h : 8 * h + 8, r, :, c],
                        start=(n == 0),
                        stop=(n == 3),
                    )
            hbank_t[(b, h)] = bank

        def haar_pe_out(b, h):
            nc.scalar.activation(
                out=ll_bf[b][:, P * h : P * (h + 1), :],
                in_=hbank_t[(b, h)][:].rearrange("p t n -> p n t"),
                func=ACT.Copy,
                scale=0.5,
            )

        def haar_v(b, h, t0=0, t1=T):
            hr, lo = haar_tiles[b]
            xv = xs[b][:].rearrange("p t (i r w) -> p t i r w", r=2, w=32)
            hv = hr[:].rearrange("p (t i) w -> p t i w", t=T)
            lv = lo[:].rearrange("p (t i) w -> p t i w", t=T)
            s = slice(8 * h, 8 * h + 8)
            nc.vector.tensor_tensor(
                out=hv[:, t0:t1, s, :], in0=xv[:, t0:t1, s, 0, :], in1=xv[:, t0:t1, s, 1, :], op=ALU.add
            )
            nc.vector.tensor_tensor(
                out=lv[:, t0:t1, s, :], in0=hv[:, t0:t1, s, 0::2], in1=hv[:, t0:t1, s, 1::2], op=ALU.add
            )

        def haar_group(b, h):
            s = slice(8 * h, 8 * h + 8)
            nc.scalar.activation(
                out=ll_bf[b][:, P * h : P * (h + 1), :],
                in_=haar_tiles[b][1][:].rearrange("p (t i) w -> p i w t", t=T)[:, s],
                func=ACT.Copy,
                scale=0.5,
            )

        def quant_ll(b):
            s = slice(NPX * b, NPX * (b + 1))
            nc.vector.quantize_mx(
                out=llc[:, s].bitcast(FP8X4), scales=lls[:, s], in_=ll_bf[b][:].rearrange("p n j -> p (n j)")
            )

        y_bf, ybank_t = {}, {}

        def conv1(b, h, bank):
            if h == 0:
                yb = work.tile([P, NPX, 4], BF16, name="y_bf", tag="y_bf", align_bytes=64)
                y_bf[b] = yb
            px = slice(NPX * b + P * h, NPX * b + P * (h + 1))
            for t in range(T):
                ch = slice(P * t, P * (t + 1))
                nc.tensor.matmul_mx(
                    out=bank[:, t, :],
                    lhsT=c1_codes[:, ch].bitcast(FP8X4),
                    lhsT_scale=c1_scales[:, ch],
                    rhs=llc[:, px].bitcast(FP8X4),
                    rhs_scale=lls[:, px],
                    start=True,
                    stop=True,
                )
            ybank_t[(b, h)] = bank

        def bias1(b, h):
            nc.vector.tensor_tensor(
                out=y_bf[b][:, P * h : P * (h + 1), :],
                in0=ybank_t[(b, h)][:].rearrange("p t n -> p n t"),
                in1=b1[:].unsqueeze(1).to_broadcast([P, P, T]),
                op=ALU.add,
            )

        def ybank_zk():
            bank = pzk.tile([P, T, P], F32, name="ybank", tag="zk")
            return bank

        def ybank_sa():
            bank = psa.tile([P, T, P], F32, name="ybank", tag="sa")
            return bank

        def quant_y(b):
            nc.vector.quantize_mx(
                out=ys[0][:, b, 16:272].bitcast(FP8X4),
                scales=sp[:, CENTER, NPX * b : NPX * (b + 1)],
                in_=y_bf[b][:].rearrange("p n j -> p (n j)"),
            )

        def shift_codes(half, dj, eng):
            bs = slice(2 * half, 2 * half + 2)
            src = ys[0][:, bs, 16:272].bitcast(I32).rearrange("p b (i w) -> p b i w", w=16)
            dst = ys[dj][:, bs, 16:272].bitcast(I32).rearrange("p b (i w) -> p b i w", w=16)
            lo, hi = max(0, -dj), min(16, 16 - dj)
            eng.tensor_copy(out=dst[:, :, :, lo:hi], in_=src[:, :, :, lo + dj : hi + dj])

        def shift_scales_w(half, dj, eng):
            px = slice(512 * half, 512 * (half + 1))
            lo, hi = max(0, -dj), min(16, 16 - dj)
            dst = sp[:, CENTER + dj, px].rearrange("p (n w) -> p n w", w=16)
            src = sp[:, CENTER, px].rearrange("p (n w) -> p n w", w=16)
            eng.tensor_copy(out=dst[:, :, lo:hi], in_=src[:, :, lo + dj : hi + dj])

        def shift_scales_h(half, dj, eng):
            px = slice(512 * half, 512 * (half + 1))
            src = sp[:, CENTER + dj, px].bitcast(I32).rearrange("p (b n) -> p b n", b=2)
            for di in (-1, 1):
                dst = sp[:, CENTER + 3 * di + dj, px].bitcast(I32).rearrange("p (b n) -> p b n", b=2)
                lo, hi = max(0, -4 * di), min(64, 64 - 4 * di)
                eng.tensor_copy(out=dst[:, :, lo:hi], in_=src[:, :, lo + 4 * di : hi + 4 * di])

        def shifts(half, eng):
            for dj in (-1, 1):
                shift_scales_w(half, dj, eng)
            for dj in (-1, 1):
                shift_codes(half, dj, nc.vector)
            for dj in (-1, 0, 1):
                shift_scales_h(half, dj, eng)

        qb_t, kb0_t, m_t, qt_t, mtt_t, ext_t = {}, {}, {}, {}, {}, {}
        kbank_t, qbank_t, qtbank_t, mtbank_t, pr_t = {}, {}, {}, {}, {}

        def ch_matmuls(bank, codes, scales, ct, half):
            ch = slice(P * ct, P * (ct + 1))
            for bb in range(2):
                b = 2 * half + bb
                nc.tensor.matmul_mx(
                    out=bank[:, NPX * bb : NPX * (bb + 1)],
                    lhsT=codes[:, ch].bitcast(FP8X4),
                    lhsT_scale=scales[:, ch],
                    rhs=ys[0][:, b, 16:272].bitcast(FP8X4),
                    rhs_scale=sp[:, CENTER, NPX * b : NPX * (b + 1)],
                    start=True,
                    stop=True,
                )

        def px_matmuls(bank, ct, half, di, dj, codes, scales):
            ch = slice(P * ct, P * (ct + 1))
            for n in range(4):
                b, r0 = 2 * half + n // 2, 8 * (n % 2)
                w0 = 16 * (r0 + 1 + di)
                px = NPX * b + 16 * r0
                nc.tensor.matmul_mx(
                    out=bank[:, P * n : P * (n + 1)],
                    lhsT=ys[dj][:, b, w0 : w0 + P].bitcast(FP8X4),
                    lhsT_scale=sp[:, CENTER + 3 * di + dj, px : px + P],
                    rhs=codes[:, ch].bitcast(FP8X4),
                    rhs_scale=scales[:, ch],
                    start=True,
                    stop=True,
                )

        def make_k(g):
            ct, half = SB_ORDER[g]
            bank = pzk.tile([P, HW], F32, name="kbank", tag="zk")
            ch_matmuls(bank, k_codes, k_scales, ct, half)
            kbank_t[g] = bank

        def copy_k(g):
            bank = kbank_t[g]
            kb0 = attn.tile([P, 2, 16, 16], BF16, name="kb0", tag="kb0")
            kb0_t[g] = kb0
            nc.scalar.copy(out=kb0[:].rearrange("p b i w -> p (b i w)"), in_=bank[:])
            nc.scalar.copy(out=kb1[g % 2][:, :, :, 3:19], in_=kb0[:])

        def make_q(g):
            ct, half = SB_ORDER[g]
            bank = pzk.tile([P, HW], F32, name="qbank", tag="zk")
            ch_matmuls(bank, q_codes, q_scales, ct, half)
            qbank_t[g] = bank

        def copy_q(g):
            bank = qbank_t[g]
            qb = attn.tile([P, HW], BF16, name="qb", tag="qb")
            qb_t[g] = qb
            nc.scalar.copy(out=qb[:], in_=bank[:])

        def make_qt(g):
            ct, half = SB_ORDER[g]
            bank = pzk.tile([P, HW], F32, name="qtbank", tag="zk")
            px_matmuls(bank, ct, half, 0, 0, q_codes, q_scales)
            qtbank_t[g] = bank

        def copy_qt(g):
            bank = qtbank_t[g]
            qt = attn.tile([P, HW], F32, name="qt", tag="qt")
            qt_t[g] = qt
            nc.scalar.copy(out=qt[:], in_=bank[:])

        def make_ext(g, stage):
            k1, k0 = kb1[g % 2], kb0_t[g]
            for which, op in enumerate((ALU.max, ALU.min)):
                hx = (hmx, hmn)[which][g % 2]
                if stage == 0:
                    tmp = attn.tile([P, 2, 16, 16], BF16, name="tmp", tag="tmp%d" % which, bufs=1)
                    nc.vector.tensor_tensor(out=tmp[:], in0=k1[:, :, :, 2:18], in1=k1[:, :, :, 4:20], op=op)
                    ext_t[which] = tmp
                elif stage == 1:
                    nc.vector.tensor_tensor(out=hx[:, :, 1:17, :], in0=ext_t[which][:], in1=k0[:], op=op)
                elif stage == 2:
                    pair = attn.tile([P, 2, 8, 16], BF16, name="pair", tag="pair%d" % which, bufs=1)
                    hp = hx[:, :, 1:17, :].rearrange("p b (i r) w -> p b i r w", r=2)
                    nc.vector.tensor_tensor(out=pair[:], in0=hp[:, :, :, 0, :], in1=hp[:, :, :, 1, :], op=op)
                    ext_t[which] = pair
                else:
                    pair = ext_t[which]
                    ext = attn.tile([P, 2, 16, 16], BF16, name="ext", tag="ext%d" % which, bufs=1)
                    ev_ = ext[:].rearrange("p b (i r) w -> p b i r w", r=2)
                    nc.vector.tensor_tensor(out=ev_[:, :, :, 0, :], in0=pair[:], in1=hx[:, :, 0:16:2, :], op=op)
                    nc.vector.tensor_tensor(out=ev_[:, :, :, 1, :], in0=pair[:], in1=hx[:, :, 3:18:2, :], op=op)
                    ext_t[(g, which)] = ext

        def make_prod(g, which):
            pr = attn.tile([P, HW], BF16, name="pr", tag="pr%d" % which, bufs=1)
            nc.vector.tensor_tensor(
                out=pr[:], in0=qb_t[g][:], in1=ext_t[(g, which)][:].rearrange("p b i w -> p (b i w)"), op=ALU.mult
            )
            pr_t[(g, which)] = pr

        def make_m(g):
            mt = attn.tile([P, HW], F32, name="mt", tag="mt", bufs=1)
            nc.vector.tensor_tensor(out=mt[:], in0=pr_t[(g, 0)][:], in1=pr_t[(g, 1)][:], op=ALU.max)
            m_t[g] = mt

        def make_mt(g):
            bank = pzk.tile([P, HW], F32, name="mtbank", tag="zk")
            for n in range(4):
                blk = slice(P * n, P * (n + 1))
                nc.tensor.transpose(bank[:, blk], m_t[g][:, blk], ident_f[:])
            mtbank_t[g] = bank

        def copy_mt(g):
            bank = mtbank_t[g]
            mtt = attn.tile([P, HW], F32, name="mtt", tag="mtt")
            mtt_t[g] = mtt
            nc.scalar.copy(out=mtt[:], in_=bank[:])

        NS = NOFF * len(SB_ORDER)
        kt_t, zd_t, z_t, e_t, v_t, ev_t, sa_t = {}, {}, {}, {}, {}, {}, {}

        def step_kt(s):
            g, j = divmod(s, NOFF)
            bank = pzk.tile([P, HW], F32, name="ktbank", tag="zk")
            px_matmuls(bank, *SB_ORDER[g], *OFFSETS[j], k_codes, k_scales)
            kt_t[s] = bank

        def step_v(s):
            g, j = divmod(s, NOFF)
            bank = pv.tile([P, HW], F32, name="vbank", tag="v")
            v_t[s] = bank
            keeper(s)
            px_matmuls(bank, *SB_ORDER[g], *OFFSETS[j], v_codes, v_scales)

        def keeper(s):
            if KEEP:
                nc.tensor.matmul_mx(
                    out=v_t[s][:, 0:KEEP],
                    lhsT=k_codes[:, 0:P].bitcast(FP8X4),
                    lhsT_scale=k_scales[:, 0:P],
                    rhs=k_codes[:, 0:KEEP].bitcast(FP8X4),
                    rhs_scale=k_scales[:, 0:KEEP],
                    start=True,
                    stop=True,
                )

        def step_qk(s):
            zd = attn.tile([P, HW], F32, name="zd", tag="zd", bufs=7)
            zd_t[s] = zd
            nc.vector.tensor_tensor(out=zd[:], in0=kt_t[s][:], in1=qt_t[s // NOFF][:], op=ALU.mult)

        def step_z(s):
            zt = attn.tile([P, HW], F32, name="zt", tag="zt", bufs=4)
            z_t[s] = zt
            eng = nc.vector if s % NOFF in V_SUB else nc.gpsimd
            eng.tensor_tensor(out=zt[:], in0=zd_t[s][:], in1=mtt_t[s // NOFF][:], op=ALU.subtract)

        def step_exp(s):
            et = attn.tile([P, HW], F32, name="et", tag="et", bufs=5)
            e_t[s] = et
            nc.scalar.activation(out=et[:], in_=z_t[s][:], func=ACT.Exp)

        def step_ev(s):
            evt = attn.tile([P, HW], F32, name="evt", tag="evt", bufs=3)
            ev_t[s] = evt
            nc.vector.tensor_tensor(out=evt[:], in0=v_t[s][:], in1=e_t[s][:], op=ALU.mult)

        def step_sa(s):
            g, j = divmod(s, NOFF)
            if j == 0:
                sbank = psa.tile([P, HW], F32, name="sbank", tag="sa")
                abank = psa.tile([P, HW], F32, name="abank", tag="sa")
                sa_t[g] = (sbank, abank)
            for bank, src in zip(sa_t[g], (e_t[s], ev_t[s])):
                for n in range(4):
                    blk = slice(P * n, P * (n + 1))
                    nc.tensor.matmul(
                        bank[:, blk],
                        lhsT=src[:, blk],
                        rhs=ident_f[:],
                        start=(j == 0 and n == 0),
                        stop=(j == NOFF - 1 and n == 3),
                        is_transpose=True,
                    )

        jobs = {}

        def at_slot(i, kind, fn, *args):
            jobs.setdefault((i, kind), []).append((fn, args))

        def run(i, kind):
            for fn, args in jobs.get((i, kind), []):
                fn(*args)

        def pipeline(i):
            if 0 <= i + L_K < NS:
                step_kt(i + L_K)
            run(i, "mx")
            if 0 <= i + L_V < NS:
                step_v(i + L_V)
            run(i, "a")
            if 0 <= i + L_X < NS:
                step_exp(i + L_X)
            if 0 <= i + L_EV < NS:
                step_ev(i + L_EV)
            if 0 <= i + L_K < NS:
                step_qk(i + L_K)
            run(i, "v")
            if 0 <= i + L_Z < NS:
                step_z(i + L_Z)
            run(i, "g")
            if 0 <= i < NS:
                step_sa(i)
            run(i, "tr")
            run(i, "a2")

        ss_t, at_t, r_t, cs_t, bn_t, rs_t, re_t, li_t = {}, {}, {}, {}, {}, {}, {}, {}

        def sums_out(g):
            ct, half = SB_ORDER[g]
            if ct not in ss_t:
                ss = attn.tile([P, 1024], F32, name="ss", tag="ss", bufs=3)
                at = attn.tile([P, 1024], F32, name="at", tag="at", bufs=3)
                ss_t[ct], at_t[ct] = ss, at
            sl = slice(HW * half, HW * (half + 1))
            nc.scalar.copy(out=ss_t[ct][:, sl], in_=sa_t[g][0][:])
            nc.scalar.copy(out=at_t[ct][:, sl], in_=sa_t[g][1][:])

        def recip(ct):
            ln = attn.tile([P, 1024], F32, name="ln", tag="ln")
            nc.scalar.activation(out=ln[:], in_=ss_t[ct][:], func=ACT.Ln)
            nc.scalar.activation(out=ln[:], in_=ln[:], func=ACT.Exp, scale=-1.0)
            r_t[ct] = ln

        def attend(ct, h):
            at = at_t[ct]
            if h == 0:
                bn = attn.tile([P, 8], F32, name="bn", tag="bn")
                bn_t[ct] = bn
            sl = slice(HW * h, HW * (h + 1))
            nc.vector.scalar_tensor_tensor(
                out=at[:, sl], in0=at[:, sl], scalar=1.0, in1=r_t[ct][:, sl], op0=ALU.mult, op1=ALU.mult,
                accum_out=bn_t[ct][:, h : h + 1],
            )

        def negmean(ct):
            bn = bn_t[ct]
            nc.vector.tensor_scalar(
                out=bn[:, 2:3], in0=bn[:, 0:1], scalar1=bn[:, 1:2], scalar2=-1.0 / 1024, op0=ALU.add, op1=ALU.mult
            )

        def squares(ct):
            bn = bn_t[ct]
            nc.scalar.activation(
                out=r_t[ct][:], in_=at_t[ct][:], func=ACT.Square, bias=bn[:, 2:3], accum_out=bn[:, 3:4]
            )

        gam = keep.tile([P, T, 2], F32, name="gam")
        bet = keep.tile([P, T], F32, name="bet")
        aa = keep.tile([P, 1], F32, name="aa")
        oma = keep.tile([P, 1], F32, name="oma")

        def load_affine():
            nc.vector.tensor_copy(out=aa[:], in_=a_b[:])
            nc.vector.tensor_copy(out=bet[:], in_=bet_b[:])
            nc.vector.tensor_copy(out=gam[:, :, 0], in_=gam_b[:])
            nc.vector.tensor_scalar(out=gam[:, :, 1], in0=gam[:, :, 0], scalar1=aa[:], scalar2=None, op0=ALU.mult)
            nc.vector.tensor_scalar(out=oma[:], in0=aa[:], scalar1=-1.0, scalar2=1.0, op0=ALU.mult, op1=ALU.add)

        def affine(ct):
            bn = bn_t[ct]
            rs = attn.tile([P, 2], F32, name="rs", tag="rs")
            rs_t[ct] = rs
            nc.gpsimd.tensor_scalar(
                out=rs[:, 0:1], in0=bn[:, 3:4], scalar1=1.0 / 1024, scalar2=1e-5, op0=ALU.mult, op1=ALU.add
            )
            nc.gpsimd.tensor_tensor(out=rs[:, 1:2], in0=rs[:, 0:1], in1=neghalf[:], op=ALU.pow)

        def affine2(ct):
            bn, rs = bn_t[ct], rs_t[ct]
            cs = attn.tile([P, 8], F32, name="cs", tag="cs")
            cs_t[ct] = cs
            nc.vector.tensor_scalar(out=cs[:, 0:2], in0=gam[:, ct, :], scalar1=rs[:, 1:2], scalar2=None, op0=ALU.mult)
            nc.vector.scalar_tensor_tensor(
                out=cs[:, 2:3], in0=bn[:, 2:3], scalar=cs[:, 0:1], in1=bet[:, ct : ct + 1], op0=ALU.mult, op1=ALU.add
            )
            nc.vector.tensor_scalar(out=cs[:, 3:4], in0=cs[:, 2:3], scalar1=aa[:], scalar2=None, op0=ALU.mult)

        out_v = out.rearrange("b (p t) h w -> t p b (h w)", t=T)

        def finish(ct, h):
            cs, at = cs_t[ct], at_t[ct]
            sl = slice(HW * h, HW * (h + 1))
            re = attn.tile([P, HW], F32, name="re", tag="re")
            li = attn.tile([P, HW], F32, name="li", tag="li")
            re_t[(ct, h)], li_t[(ct, h)] = re, li
            nc.scalar.activation(out=re[:], in_=at[:, sl], func=ACT.Relu, scale=cs[:, 0:1], bias=cs[:, 2:3])
            if ct == 3 or LI_V:
                nc.vector.tensor_scalar(
                    out=li[:], in0=at[:, sl], scalar1=cs[:, 1:2], scalar2=cs[:, 3:4], op0=ALU.mult, op1=ALU.add
                )
            else:
                nc.scalar.activation(out=li[:], in_=at[:, sl], func=ACT.Identity, scale=cs[:, 1:2], bias=cs[:, 3:4])

        def finish2(ct, h):
            re, li = re_t[(ct, h)], li_t[(ct, h)]
            nc.vector.scalar_tensor_tensor(out=re[:], in0=re[:], scalar=oma[:], in1=li[:], op0=ALU.mult, op1=ALU.add)
            nc.sync.dma_start(out=out_v[ct][:, 2 * h : 2 * h + 2, :], in_=re[:].rearrange("p (b n) -> p b n", b=2))

        vcopy = nc.vector.tensor_copy
        acopy = nc.scalar.copy
        haar_alloc(0)
        haar_alloc(1)
        c1_tr = tr_weight(as_words(raw_c1), "c1", psa, "sa")
        haar_pe(1, 0)
        k_tr = tr_weight(as_words(raw_k), "wk", pv, "v")
        q_tr = tr_weight(as_words(raw_q), "wq", psa, "sa")
        copy_weight(c1_tr, (acopy, vcopy))
        haar_v(0, 0, 0, 2)
        haar_v(0, 0, 2, 4)
        haar_v(0, 1)
        c1_codes, c1_scales = quant_weight(c1_tr)
        haar_v(1, 1)
        haar_group(0, 0)
        haar_group(0, 1)
        haar_pe_out(1, 0)
        haar_group(1, 1)
        quant_ll(0)
        wv_bf = raws.tile([P, T, 512], BF16, name="wv_bf")

        def wv_product(t):
            nc.vector.tensor_tensor(out=wv_bf[:, t, :], in0=raw_vb[:, t, :].bitcast(FP8), in1=vscale[:], op=ALU.mult)

        wv_product(0)
        quant_ll(1)
        copy_weight(k_tr, (acopy, acopy))
        for b in range(2):
            for h in range(2):
                conv1(b, h, ybank_zk())
        bias1(0, 0)
        bias1(0, 1)
        quant_y(0)
        bias1(1, 0)
        bias1(1, 1)
        quant_y(1)
        k_codes, k_scales = quant_weight(k_tr)
        copy_weight(q_tr, (acopy, acopy))
        for t in range(1, T):
            wv_product(t)
        make_k(0)
        copy_k(0)
        q_codes, q_scales = quant_weight(q_tr)
        make_q(0)
        copy_q(0)
        make_qt(0)
        v_tr = tr_weight(as_words(wv_bf), "wv", psa, "sa")
        copy_qt(0)
        for stage in range(4):
            make_ext(0, stage)
        make_prod(0, 0)
        make_prod(0, 1)
        make_m(0)
        make_mt(0)
        copy_weight(v_tr, (acopy, vcopy))
        copy_mt(0)
        shift_scales_h(0, 0, nc.vector)
        for dj in (1, -1):
            shift_scales_w(0, dj, nc.vector)
        v_codes, v_scales = quant_weight(v_tr)
        for dj in (1, -1):
            shift_codes(0, dj, nc.vector)
            shift_scales_h(0, dj, nc.vector)
        for b in (2, 3):
            s = 6 * (b - 2)
            at_slot(s, "mx", haar_alloc, b)
            for h in range(2):
                if 2 * (b - 2) + h + 1 < N_PE_HAAR:
                    at_slot(s + h, "mx", haar_pe, b, h)
                    at_slot(s + h + 1, "a", haar_pe_out, b, h)
                else:
                    at_slot(s + h, "v", haar_v, b, h)
                    at_slot(s + h + 1, "a", haar_group, b, h)
            at_slot(s + 3, "v", quant_ll, b)
            for h in range(2):
                at_slot(s + 4 + h, "mx", lambda b_, h_: conv1(b_, h_, ybank_zk()), b, h)
                at_slot(s + 5 + h, "v", bias1, b, h)
            at_slot(s + 7, "v", quant_y, b)
        for dj in (-1, 1):
            at_slot(14, "v", shift_scales_w, 1, dj, nc.vector)
            at_slot(14, "v", shift_codes, 1, dj, nc.vector)
        for dj in (-1, 0, 1):
            at_slot(15, "v", shift_scales_h, 1, dj, nc.vector)
        at_slot(16, "v", load_affine)

        done = set()
        for g, (ct, half) in enumerate(SB_ORDER):
            s0 = NOFF * g
            if g > 0:
                at_slot(max(0, s0 + E_K), "mx", make_k, g)
                at_slot(max(0, s0 + E_K), "a", copy_k, g)
                at_slot(max(0, s0 + E_QT), "mx", make_qt, g)
                at_slot(max(0, s0 + E_QT), "a", copy_qt, g)
                at_slot(max(0, s0 + E_Q), "mx", make_q, g)
                at_slot(max(0, s0 + E_Q), "a", copy_q, g)
                for n in range(4):
                    at_slot(max(0, s0 + E_CH), "v", make_ext, g, n)
                at_slot(max(0, s0 + E_CH), "v", make_prod, g, 0)
                at_slot(max(0, s0 + E_CH), "v", make_prod, g, 1)
                at_slot(max(0, s0 + E_CH), "v", make_m, g)
                at_slot(max(0, s0 + E_MT), "tr", make_mt, g)
                at_slot(max(0, s0 + E_MT), "a2", copy_mt, g)
            e0 = s0 + NOFF
            at_slot(e0, "a", sums_out, g)
            if ct in done:
                f = (lambda n, e0=e0: e0 + n)
                at_slot(f(F_LN), "a", recip, ct)
                at_slot(f(F_A), "v", attend, ct, 0)
                at_slot(f(F_A), "v", attend, ct, 1)
                at_slot(f(F_A), "v", negmean, ct)
                at_slot(f(F_SQ), "a", squares, ct)
                at_slot(f(F_RS), "g", affine, ct)
                at_slot(f(F_CS), "v", affine2, ct)
                at_slot(f(F_R), "a", finish, ct, 0)
                at_slot(f(F_R + 1), "a", finish, ct, 1)
                at_slot(f(F_O), "v", finish2, ct, 0)
                at_slot(f(F_O), "v", finish2, ct, 1)
            done.add(ct)
        for i in range(-L_K, NS + 25):
            pipeline(i)
